import numpy as np
import ml_dtypes


def mxq(x, axis, fmt="e4m3"):
    dtype, down = {"e4m3": (ml_dtypes.float8_e4m3fn, 7), "e5m2": (ml_dtypes.float8_e5m2, 14)}[fmt]
    v = np.moveaxis(np.asarray(x, np.float32).astype(ml_dtypes.bfloat16).astype(np.float64), axis, -1)
    blocks = v.reshape(v.shape[:-1] + (-1, 32))
    amax = np.abs(blocks).max(-1, keepdims=True)
    byte = np.maximum(np.where(amax > 0, np.frexp(amax)[1] - 1 + 127, 0) - down, 1)
    scale = np.exp2(byte - 127.0)
    codes = (blocks / scale).astype(np.float32).astype(dtype).astype(np.float64)
    return np.moveaxis((codes * scale).reshape(v.shape), -1, axis)


WIDE = False


def mx_kscale(k):
    if not WIDE:
        return np.ones(k)
    levels = np.array([30, -30])
    if k % 512:
        return np.exp2(np.random.permutation(np.resize(levels, k // 32))).repeat(32)
    a = np.empty((k // 512, 16))
    for p in range(k // 512):
        a[p, :8] = np.random.permutation(np.resize(levels, 8))
        for g in range(8):
            far = levels[np.abs(levels - a[p, g]) >= 10]
            a[p, g + 8] = far[np.random.randint(len(far))]
    return np.exp2(a.ravel()).repeat(32)


BF16 = ml_dtypes.bfloat16


def bf(x):
    return np.asarray(x, np.float32).astype(BF16)


def f64(x):
    return np.asarray(x).astype(np.float64)


B, HH, WW, C, NH, KD, WS, SS = 1, 64, 64, 512, 8, 64, 8, 4
GH, GW, T, F = HH // WS, WW // WS, WS * WS, NH * KD
N = B * GH * GW


def setup_inputs():
    s = mx_kscale(F).reshape(NH, KD)
    return {"attn_ctx": bf(np.random.standard_normal((N, T, NH, KD)) * 0.4 * s),
            "x": bf(np.random.standard_normal((B, HH, WW, C))),
            "wo": bf(np.random.standard_normal((NH, KD, C)) * 2.0 / np.sqrt(F) / s[:, :, None]),
            "bo": bf(np.random.standard_normal(C) * 0.3)}


def reference(attn_ctx, x, wo, bo):
    o = f64(attn_ctx).reshape(N * T, F)
    proj = (mxq(o, 1, "e5m2") @ mxq(f64(wo).reshape(F, C), 0, "e4m3")) + f64(bo)
    merged = proj.reshape(B, GH, GW, WS, WS, C).swapaxes(2, 3).reshape(B, HH, WW, C)
    merged = np.roll(merged, shift=(SS, SS), axis=(1, 2))
    return f64(x) + merged

@@ -1,0 +1,182 @@
+from contextlib import ExitStack
+
+import concourse.mybir as mybir
+from concourse.masks import make_identity
+
+FLOPS = 2 * 4096 * 512 * 512
+
+F32 = mybir.dt.float32
+BF16 = mybir.dt.bfloat16
+U32 = mybir.dt.uint32
+U8 = mybir.dt.uint8
+E5M2X4 = mybir.dt.float8_e5m2_x4
+E4M3X4 = mybir.dt.float8_e4m3fn_x4
+ADD = mybir.AluOpType.add
+IDENTITY = mybir.ActivationFunctionType.Identity
+
+P = 128
+BLOCKS = 8
+ORDER = [7, 0, 1, 2, 3, 4, 5, 6]
+
+
+def pixel_runs(g):
+    if g < 7:
+        return [(0, 128, 512 * g + 256)]
+    return [(0, 64, 3840), (64, 128, 0)]
+
+
+def tile_windowattentionblock_pb_kernel(tc, attn_ctx, x, wo, bo, out):
+    nc = tc.nc
+    a_rows = attn_ctx.rearrange("n t h d -> (n t) (h d)")
+    x_rows = x.rearrange("b i j c -> (b i j) c")
+    o_rows = out.rearrange("b i j c -> (b i j) c")
+    w_rows = wo.rearrange("h d c -> (h d) c")
+
+    with ExitStack() as ctx:
+        keep = ctx.enter_context(tc.tile_pool(name="keep", bufs=1))
+        work = ctx.enter_context(tc.tile_pool(name="work", bufs=3))
+        ps_a = ctx.enter_context(tc.psum_pool(name="ps_a", bufs=2))
+        ps_b = ctx.enter_context(tc.psum_pool(name="ps_b", bufs=3))
+        ps_c = ctx.enter_context(tc.psum_pool(name="ps_c", bufs=3))
+        ctx.enter_context(tc.manual_schedule())
+
+        a_sb = {}
+        x_sb = {}
+        o_sb = {}
+        for g in ORDER:
+            a_sb[g] = keep.tile([P, 2048], BF16, name="a_sb%d" % g)
+            x_sb[g] = keep.tile([P, 4, 512], BF16, name="x_sb%d" % g)
+            o_sb[g] = keep.tile([P, 4, 512], F32, name="o_sb%d" % g)
+        w_raw = keep.tile([P, 4, 512], BF16, name="w_raw")
+        b_col = keep.tile([P, 4], BF16, name="b_col")
+
+        def load_a(g):
+            nc.sync.dma_start(
+                out=a_sb[g][:],
+                in_=a_rows[512 * g : 512 * (g + 1), :].rearrange("(p s) k -> p (s k)", s=4),
+            )
+
+        def load_x(g):
+            for q0, q1, pix in pixel_runs(g):
+                nc.sync.dma_start(
+                    out=x_sb[g][q0:q1, :, :],
+                    in_=x_rows[pix : pix + 4 * (q1 - q0), :].rearrange("(q s) c -> q s c", s=4),
+                )
+
+        with nc.allow_non_contiguous_dma(reason="512 bias values, one to a partition"):
+            nc.scalar.dma_start(out=b_col[:], in_=bo.rearrange("(t p) -> p t", p=P))
+        load_a(ORDER[0])
+        nc.sync.dma_start(out=w_raw[:], in_=w_rows.rearrange("(p j) c -> p j c", j=4))
+        load_a(ORDER[1])
+        for i in range(BLOCKS):
+            load_x(ORDER[i])
+            if i + 2 < BLOCKS:
+                load_a(ORDER[i + 2])
+
+        ident = keep.tile([P, P], F32, name="ident")
+        make_identity(nc, ident[:])
+        perm = keep.tile([P, P], F32, name="perm")
+        src = ident[:].rearrange("p (a t h) -> p t a h", a=8, t=8, h=2)
+        dst = perm[:].rearrange("p (t a h) -> p t a h", t=8, a=8, h=2)
+        nc.vector.tensor_copy(out=dst[:, :, :, 1], in_=src[:, :, :, 0])
+        nc.vector.tensor_copy(out=dst[:, :, 1:8, 0], in_=src[:, :, 0:7, 1])
+        nc.vector.tensor_copy(out=dst[:, :, 0, 0], in_=src[:, :, 7, 1])
+
+        warm_in = keep.tile([P, 1], F32, name="warm_in")
+        warm_out = keep.tile([P, 1], F32, name="warm_out")
+        nc.gpsimd.memset(warm_in[:], 0.0)
+        nc.scalar.activation(out=warm_out[:], in_=warm_in[:], func=IDENTITY)
+
+        w_grouped = keep.tile([P, 512, 4], BF16, name="w_grouped", align_bytes=64)
+        w_codes = keep.tile([P, 512], U32, name="w_codes", align_bytes=64)
+        w_scales = keep.tile([P, 512], U8, name="w_scales", align_bytes=64)
+
+        def prepare_w():
+            nc.vector.tensor_copy(out=w_grouped[:], in_=w_raw[:].rearrange("p j c -> p c j"))
+            nc.vector.quantize_mx(
+                out=w_codes[:].bitcast(E4M3X4),
+                scales=w_scales[:],
+                in_=w_grouped[:].rearrange("p c j -> p (c j)"),
+            )
+
+        grouped = {}
+        codes = {}
+        scales = {}
+        y_sb = {}
+
+        def stage_a(g):
+            words = a_sb[g][:].bitcast(F32)
+            grouped[g] = work.tile([P, 2048], BF16, name="grouped", align_bytes=64)
+            gw = grouped[g][:].bitcast(F32)
+            for h in range(2):
+                xt = ps_a.tile([P, 2, 2, P], F32, name="xt")
+                for a in range(2):
+                    s = 2 * h + a
+                    for u in range(2):
+                        nc.tensor.transpose(
+                            xt[:, a, u, :], words[:, 256 * s + u : 256 * (s + 1) : 2], perm[:]
+                        )
+                dst_w = gw[:, 512 * h : 512 * (h + 1)].rearrange("p (a q u) -> p a q u", a=2, u=2)
+                src_w = xt[:].rearrange("p a u q -> p a q u")
+                if h == 0:
+                    nc.scalar.copy(out=dst_w, in_=src_w)
+                else:
+                    nc.vector.tensor_copy(out=dst_w, in_=src_w)
+
+        def quantise(g):
+            codes[g] = work.tile([P, 512], U32, name="codes", align_bytes=64)
+            scales[g] = work.tile([P, 512], U8, name="scales", align_bytes=64)
+            nc.vector.quantize_mx(
+                out=codes[g][:].bitcast(E5M2X4), scales=scales[g][:], in_=grouped[g][:]
+            )
+
+        def stage_b(g):
+            y_sb[g] = work.tile([P, 4, 512], F32, name="y_sb")
+            for t in range(4):
+                cols = slice(P * t, P * (t + 1))
+                y_ps = ps_b.tile([P, 512], F32, name="y_ps")
+                nc.tensor.matmul_mx(
+                    out=y_ps[:],
+                    lhsT=w_codes[:, cols].bitcast(E4M3X4),
+                    lhsT_scale=w_scales[:, cols],
+                    rhs=codes[g][:].bitcast(E5M2X4),
+                    rhs_scale=scales[g][:],
+                    start=True,
+                    stop=True,
+                )
+                nc.scalar.activation(
+                    out=y_sb[g][:, t, :], in_=y_ps[:], func=IDENTITY, bias=b_col[:, t : t + 1], scale=1.0
+                )
+
+        def stage_c(g, last):
+            for s in range(4):
+                o_ps = ps_c.tile([P, 512], F32, name="o_ps")
+                for t in range(4):
+                    nc.tensor.transpose(
+                        o_ps[:, P * t : P * (t + 1)], y_sb[g][:, t, P * s : P * (s + 1)], ident[:]
+                    )
+                nc.vector.tensor_tensor(out=o_sb[g][:, s, :], in0=o_ps[:], in1=x_sb[g][:, s, :], op=ADD)
+                if last:
+                    for q0, q1, pix in pixel_runs(g):
+                        nc.sync.dma_start(
+                            out=o_rows[pix : pix + 4 * (q1 - q0), :].rearrange("(q s) c -> q s c", s=4)[:, s, :],
+                            in_=o_sb[g][q0:q1, s, :],
+                        )
+            if not last:
+                for q0, q1, pix in pixel_runs(g):
+                    nc.sync.dma_start(
+                        out=o_rows[pix : pix + 4 * (q1 - q0), :].rearrange("(q s) c -> q s c", s=4),
+                        in_=o_sb[g][q0:q1, :, :],
+                    )
+
+        for i in range(BLOCKS + 2):
+            if i == 1:
+                prepare_w()
+            if 1 <= i <= BLOCKS:
+                quantise(ORDER[i - 1])
+            if i < BLOCKS:
+                stage_a(ORDER[i])
+            if 1 <= i <= BLOCKS:
+                stage_b(ORDER[i - 1])
+            if i >= 2:
+                stage_c(ORDER[i - 2], i - 2 == BLOCKS - 1)

@@ -16,7 +16,9 @@ IDENTITY = mybir.ActivationFunctionType.Identity
 
 P = 128
 BLOCKS = 8
+PAIRS = 4
 ORDER = [7, 0, 1, 2, 3, 4, 5, 6]
+LOADS = ["a0", "a1", "w", "x1", "a2", "a3", "x0", "x3", "a4", "a5", "x2", "x5", "a6", "a7", "x4", "x7", "x6"]
 
 
 def pixel_runs(g):
@@ -34,44 +36,45 @@ def tile_windowattentionblock_pb_kernel(tc, attn_ctx, x, wo, bo, out):
 
     with ExitStack() as ctx:
         keep = ctx.enter_context(tc.tile_pool(name="keep", bufs=1))
-        work = ctx.enter_context(tc.tile_pool(name="work", bufs=3))
-        ps_a = ctx.enter_context(tc.psum_pool(name="ps_a", bufs=2))
-        ps_b = ctx.enter_context(tc.psum_pool(name="ps_b", bufs=3))
+        work = ctx.enter_context(tc.tile_pool(name="work", bufs=4))
+        ybuf = ctx.enter_context(tc.tile_pool(name="ybuf", bufs=2))
+        ps_a = ctx.enter_context(tc.psum_pool(name="ps_a", bufs=3))
+        ps_b = ctx.enter_context(tc.psum_pool(name="ps_b", bufs=2))
         ps_c = ctx.enter_context(tc.psum_pool(name="ps_c", bufs=3))
         ctx.enter_context(tc.manual_schedule())
 
         a_sb = {}
         x_sb = {}
         o_sb = {}
-        for g in ORDER:
-            a_sb[g] = keep.tile([P, 2048], BF16, name="a_sb%d" % g)
-            x_sb[g] = keep.tile([P, 4, 512], BF16, name="x_sb%d" % g)
-            o_sb[g] = keep.tile([P, 4, 512], F32, name="o_sb%d" % g)
+        xb_sb = {}
+        for i in range(BLOCKS):
+            a_sb[i] = keep.tile([P, 2048], BF16, name="a_sb%d" % i)
+            x_sb[i] = keep.tile([P, 4, 512], BF16, name="x_sb%d" % i)
+            o_sb[i] = keep.tile([P, 4, 512], F32, name="o_sb%d" % i)
+            if i % 2 == 1:
+                xb_sb[i] = keep.tile([P, 4, 512], F32, name="xb_sb%d" % i)
         w_raw = keep.tile([P, 4, 512], BF16, name="w_raw")
         b_col = keep.tile([P, 4], BF16, name="b_col")
 
-        def load_a(g):
-            nc.sync.dma_start(
-                out=a_sb[g][:],
-                in_=a_rows[512 * g : 512 * (g + 1), :].rearrange("(p s) k -> p (s k)", s=4),
-            )
-
-        def load_x(g):
-            for q0, q1, pix in pixel_runs(g):
-                nc.sync.dma_start(
-                    out=x_sb[g][q0:q1, :, :],
-                    in_=x_rows[pix : pix + 4 * (q1 - q0), :].rearrange("(q s) c -> q s c", s=4),
-                )
-
         with nc.allow_non_contiguous_dma(reason="512 bias values, one to a partition"):
             nc.scalar.dma_start(out=b_col[:], in_=bo.rearrange("(t p) -> p t", p=P))
-        load_a(ORDER[0])
-        nc.sync.dma_start(out=w_raw[:], in_=w_rows.rearrange("(p j) c -> p j c", j=4))
-        load_a(ORDER[1])
-        for i in range(BLOCKS):
-            load_x(ORDER[i])
-            if i + 2 < BLOCKS:
-                load_a(ORDER[i + 2])
+        for what in LOADS:
+            if what == "w":
+                nc.sync.dma_start(out=w_raw[:], in_=w_rows.rearrange("(p j) c -> p j c", j=4))
+            elif what.startswith("a"):
+                i = int(what[1:])
+                g = ORDER[i]
+                nc.sync.dma_start(
+                    out=a_sb[i][:],
+                    in_=a_rows[512 * g : 512 * (g + 1), :].rearrange("(p s) k -> p (s k)", s=4),
+                )
+            else:
+                i = int(what[1:])
+                for q0, q1, pix in pixel_runs(ORDER[i]):
+                    nc.sync.dma_start(
+                        out=x_sb[i][q0:q1, :, :],
+                        in_=x_rows[pix : pix + 4 * (q1 - q0), :].rearrange("(q s) c -> q s c", s=4),
+                    )
 
         ident = keep.tile([P, P], F32, name="ident")
         make_identity(nc, ident[:])
@@ -81,6 +84,8 @@ def tile_windowattentionblock_pb_kernel(tc, attn_ctx, x, wo, bo, out):
         nc.vector.tensor_copy(out=dst[:, :, :, 1], in_=src[:, :, :, 0])
         nc.vector.tensor_copy(out=dst[:, :, 1:8, 0], in_=src[:, :, 0:7, 1])
         nc.vector.tensor_copy(out=dst[:, :, 0, 0], in_=src[:, :, 7, 1])
+        ident_bf = keep.tile([P, P], BF16, name="ident_bf")
+        nc.vector.tensor_copy(out=ident_bf[:], in_=ident[:])
 
         warm_in = keep.tile([P, 1], F32, name="warm_in")
         warm_out = keep.tile([P, 1], F32, name="warm_out")
@@ -90,6 +95,7 @@ def tile_windowattentionblock_pb_kernel(tc, attn_ctx, x, wo, bo, out):
         w_grouped = keep.tile([P, 512, 4], BF16, name="w_grouped", align_bytes=64)
         w_codes = keep.tile([P, 512], U32, name="w_codes", align_bytes=64)
         w_scales = keep.tile([P, 512], U8, name="w_scales", align_bytes=64)
+        b_bc = keep.tile([P, 512], F32, name="b_bc")
 
         def prepare_w():
             nc.vector.tensor_copy(out=w_grouped[:], in_=w_raw[:].rearrange("p j c -> p c j"))
@@ -99,15 +105,31 @@ def tile_windowattentionblock_pb_kernel(tc, attn_ctx, x, wo, bo, out):
                 in_=w_grouped[:].rearrange("p c j -> p (c j)"),
             )
 
+        def spread_bias():
+            bb_ps = ps_c.tile([P, 512], F32, name="o_ps")
+            for t in range(4):
+                nc.tensor.matmul(
+                    out=bb_ps[:, P * t : P * (t + 1)],
+                    lhsT=b_col[:, t : t + 1].to_broadcast([P, P]),
+                    rhs=ident_bf[:],
+                    start=True,
+                    stop=True,
+                )
+            nc.scalar.copy(out=b_bc[:], in_=bb_ps[:])
+
+        def add_bias_to_x(i):
+            for s in range(4):
+                nc.gpsimd.tensor_tensor(out=xb_sb[i][:, s, :], in0=x_sb[i][:, s, :], in1=b_bc[:], op=ADD)
+
         grouped = {}
         codes = {}
         scales = {}
         y_sb = {}
 
-        def stage_a(g):
-            words = a_sb[g][:].bitcast(F32)
-            grouped[g] = work.tile([P, 2048], BF16, name="grouped", align_bytes=64)
-            gw = grouped[g][:].bitcast(F32)
+        def stage_a(i):
+            words = a_sb[i][:].bitcast(F32)
+            grouped[i] = work.tile([P, 2048], BF16, name="grouped", align_bytes=64)
+            gw = grouped[i][:].bitcast(F32)
             for h in range(2):
                 xt = ps_a.tile([P, 2, 2, P], F32, name="xt")
                 for a in range(2):
@@ -116,67 +138,93 @@ def tile_windowattentionblock_pb_kernel(tc, attn_ctx, x, wo, bo, out):
                         nc.tensor.transpose(
                             xt[:, a, u, :], words[:, 256 * s + u : 256 * (s + 1) : 2], perm[:]
                         )
-                dst_w = gw[:, 512 * h : 512 * (h + 1)].rearrange("p (a q u) -> p a q u", a=2, u=2)
-                src_w = xt[:].rearrange("p a u q -> p a q u")
-                if h == 0:
-                    nc.scalar.copy(out=dst_w, in_=src_w)
-                else:
-                    nc.vector.tensor_copy(out=dst_w, in_=src_w)
+                nc.scalar.copy(
+                    out=gw[:, 512 * h : 512 * (h + 1)].rearrange("p (a q u) -> p a q u", a=2, u=2),
+                    in_=xt[:].rearrange("p a u q -> p a q u"),
+                )
 
-        def quantise(g):
-            codes[g] = work.tile([P, 512], U32, name="codes", align_bytes=64)
-            scales[g] = work.tile([P, 512], U8, name="scales", align_bytes=64)
+        def quantise(i):
+            codes[i] = work.tile([P, 512], U32, name="codes", align_bytes=64)
+            scales[i] = work.tile([P, 512], U8, name="scales", align_bytes=64)
             nc.vector.quantize_mx(
-                out=codes[g][:].bitcast(E5M2X4), scales=scales[g][:], in_=grouped[g][:]
+                out=codes[i][:].bitcast(E5M2X4), scales=scales[i][:], in_=grouped[i][:]
             )
 
-        def stage_b(g):
-            y_sb[g] = work.tile([P, 4, 512], F32, name="y_sb")
-            for t in range(4):
-                cols = slice(P * t, P * (t + 1))
-                y_ps = ps_b.tile([P, 512], F32, name="y_ps")
-                nc.tensor.matmul_mx(
-                    out=y_ps[:],
-                    lhsT=w_codes[:, cols].bitcast(E4M3X4),
-                    lhsT_scale=w_scales[:, cols],
-                    rhs=codes[g][:].bitcast(E5M2X4),
-                    rhs_scale=scales[g][:],
-                    start=True,
-                    stop=True,
-                )
-                nc.scalar.activation(
-                    out=y_sb[g][:, t, :], in_=y_ps[:], func=IDENTITY, bias=b_col[:, t : t + 1], scale=1.0
-                )
+        def store(i, s):
+            for q0, q1, pix in pixel_runs(ORDER[i]):
+                rows = o_rows[pix : pix + 4 * (q1 - q0), :].rearrange("(q s) c -> q s c", s=4)
+                if s is None:
+                    nc.sync.dma_start(out=rows, in_=o_sb[i][q0:q1, :, :])
+                else:
+                    nc.sync.dma_start(out=rows[:, s, :], in_=o_sb[i][q0:q1, s, :])
 
-        def stage_c(g, last):
+        def tokens_stationary(i, s, fine):
+            cols = slice(P * s, P * (s + 1))
+            o_ps = ps_c.tile([P, 512], F32, name="o_ps")
+            nc.tensor.matmul_mx(
+                out=o_ps[:],
+                lhsT=codes[i][:, cols].bitcast(E5M2X4),
+                lhsT_scale=scales[i][:, cols],
+                rhs=w_codes[:].bitcast(E4M3X4),
+                rhs_scale=w_scales[:],
+                start=True,
+                stop=True,
+            )
+            nc.vector.tensor_tensor(out=o_sb[i][:, s, :], in0=o_ps[:], in1=xb_sb[i][:, s, :], op=ADD)
+            if fine:
+                store(i, s)
+
+        def weights_stationary(i, t):
+            cols = slice(P * t, P * (t + 1))
+            y_ps = ps_b.tile([P, 512], F32, name="y_ps")
+            nc.tensor.matmul_mx(
+                out=y_ps[:],
+                lhsT=w_codes[:, cols].bitcast(E4M3X4),
+                lhsT_scale=w_scales[:, cols],
+                rhs=codes[i][:].bitcast(E5M2X4),
+                rhs_scale=scales[i][:],
+                start=True,
+                stop=True,
+            )
+            nc.scalar.activation(
+                out=y_sb[i][:, t, :], in_=y_ps[:], func=IDENTITY, bias=b_col[:, t : t + 1], scale=1.0
+            )
+
+        def turn_back(i, fine):
             for s in range(4):
                 o_ps = ps_c.tile([P, 512], F32, name="o_ps")
                 for t in range(4):
                     nc.tensor.transpose(
-                        o_ps[:, P * t : P * (t + 1)], y_sb[g][:, t, P * s : P * (s + 1)], ident[:]
+                        o_ps[:, P * t : P * (t + 1)], y_sb[i][:, t, P * s : P * (s + 1)], ident[:]
                     )
-                nc.vector.tensor_tensor(out=o_sb[g][:, s, :], in0=o_ps[:], in1=x_sb[g][:, s, :], op=ADD)
-                if last:
-                    for q0, q1, pix in pixel_runs(g):
-                        nc.sync.dma_start(
-                            out=o_rows[pix : pix + 4 * (q1 - q0), :].rearrange("(q s) c -> q s c", s=4)[:, s, :],
-                            in_=o_sb[g][q0:q1, s, :],
-                        )
-            if not last:
-                for q0, q1, pix in pixel_runs(g):
-                    nc.sync.dma_start(
-                        out=o_rows[pix : pix + 4 * (q1 - q0), :].rearrange("(q s) c -> q s c", s=4),
-                        in_=o_sb[g][q0:q1, :, :],
-                    )
+                nc.vector.tensor_tensor(out=o_sb[i][:, s, :], in0=o_ps[:], in1=x_sb[i][:, s, :], op=ADD)
+                if fine:
+                    store(i, s)
+            if not fine:
+                store(i, None)
 
-        for i in range(BLOCKS + 2):
-            if i == 1:
-                prepare_w()
-            if 1 <= i <= BLOCKS:
-                quantise(ORDER[i - 1])
-            if i < BLOCKS:
-                stage_a(ORDER[i])
-            if 1 <= i <= BLOCKS:
-                stage_b(ORDER[i - 1])
-            if i >= 2:
-                stage_c(ORDER[i - 2], i - 2 == BLOCKS - 1)
+        stage_a(0)
+        spread_bias()
+        stage_a(1)
+        for i in range(1, BLOCKS, 2):
+            add_bias_to_x(i)
+        prepare_w()
+        quantise(0)
+        quantise(1)
+        stage_a(2)
+        stage_a(3)
+        for j in range(PAIRS):
+            fine = j == PAIRS - 1
+            y_sb[2 * j] = ybuf.tile([P, 4, 512], F32, name="y_sb")
+            for r in range(4):
+                tokens_stationary(2 * j + 1, r, fine)
+                weights_stationary(2 * j, r)
+            if not fine:
+                store(2 * j + 1, None)
+            if j + 1 < PAIRS:
+                quantise(2 * j + 2)
+                quantise(2 * j + 3)
+            if j + 2 < PAIRS:
+                stage_a(2 * j + 4)
+                stage_a(2 * j + 5)
+            turn_back(2 * j, fine)

@@ -119,7 +119,7 @@ def tile_windowattentionblock_pb_kernel(tc, attn_ctx, x, wo, bo, out):
 
         def add_bias_to_x(i):
             for s in range(4):
-                nc.gpsimd.tensor_tensor(out=xb_sb[i][:, s, :], in0=x_sb[i][:, s, :], in1=b_bc[:], op=ADD)
+                nc.vector.tensor_tensor(out=xb_sb[i][:, s, :], in0=x_sb[i][:, s, :], in1=b_bc[:], op=ADD)
 
         grouped = {}
         codes = {}
@@ -206,11 +206,10 @@ def tile_windowattentionblock_pb_kernel(tc, attn_ctx, x, wo, bo, out):
         stage_a(0)
         spread_bias()
         stage_a(1)
-        for i in range(1, BLOCKS, 2):
-            add_bias_to_x(i)
         prepare_w()
         quantise(0)
         quantise(1)
+        add_bias_to_x(1)
         stage_a(2)
         stage_a(3)
         for j in range(PAIRS):
@@ -224,6 +223,7 @@ def tile_windowattentionblock_pb_kernel(tc, attn_ctx, x, wo, bo, out):
             if j + 1 < PAIRS:
                 quantise(2 * j + 2)
                 quantise(2 * j + 3)
+                add_bias_to_x(2 * j + 3)
             if j + 2 < PAIRS:
                 stage_a(2 * j + 4)
                 stage_a(2 * j + 5)

@@ -119,7 +119,7 @@ def tile_windowattentionblock_pb_kernel(tc, attn_ctx, x, wo, bo, out):
 
         def add_bias_to_x(i):
             for s in range(4):
-                nc.vector.tensor_tensor(out=xb_sb[i][:, s, :], in0=x_sb[i][:, s, :], in1=b_bc[:], op=ADD)
+                nc.gpsimd.tensor_tensor(out=xb_sb[i][:, s, :], in0=x_sb[i][:, s, :], in1=b_bc[:], op=ADD)
 
         grouped = {}
         codes = {}
@@ -170,7 +170,7 @@ def tile_windowattentionblock_pb_kernel(tc, attn_ctx, x, wo, bo, out):
                 start=True,
                 stop=True,
             )
-            nc.vector.tensor_tensor(out=o_sb[i][:, s, :], in0=o_ps[:], in1=xb_sb[i][:, s, :], op=ADD)
+            nc.vector.tensor_tensor(out=o_sb[i][:, s, :], in0=xb_sb[i][:, s, :], in1=o_ps[:], op=ADD)
             if fine:
                 store(i, s)
 
@@ -197,7 +197,7 @@ def tile_windowattentionblock_pb_kernel(tc, attn_ctx, x, wo, bo, out):
                     nc.tensor.transpose(
                         o_ps[:, P * t : P * (t + 1)], y_sb[i][:, t, P * s : P * (s + 1)], ident[:]
                     )
-                nc.vector.tensor_tensor(out=o_sb[i][:, s, :], in0=o_ps[:], in1=x_sb[i][:, s, :], op=ADD)
+                nc.vector.tensor_tensor(out=o_sb[i][:, s, :], in0=x_sb[i][:, s, :], in1=o_ps[:], op=ADD)
                 if fine:
                     store(i, s)
             if not fine:
@@ -206,10 +206,11 @@ def tile_windowattentionblock_pb_kernel(tc, attn_ctx, x, wo, bo, out):
         stage_a(0)
         spread_bias()
         stage_a(1)
+        for i in range(1, BLOCKS, 2):
+            add_bias_to_x(i)
         prepare_w()
         quantise(0)
         quantise(1)
-        add_bias_to_x(1)
         stage_a(2)
         stage_a(3)
         for j in range(PAIRS):
@@ -223,7 +224,6 @@ def tile_windowattentionblock_pb_kernel(tc, attn_ctx, x, wo, bo, out):
             if j + 1 < PAIRS:
                 quantise(2 * j + 2)
                 quantise(2 * j + 3)
-                add_bias_to_x(2 * j + 3)
             if j + 2 < PAIRS:
                 stage_a(2 * j + 4)
                 stage_a(2 * j + 5)

@@ -18,7 +18,7 @@ P = 128
 BLOCKS = 8
 PAIRS = 4
 ORDER = [7, 0, 1, 2, 3, 4, 5, 6]
-LOADS = ["a0", "a1", "w", "x1", "a2", "a3", "x0", "x3", "a4", "a5", "x2", "x5", "a6", "a7", "x4", "x7", "x6"]
+LOADS = ["w", "x1", "a0", "a1", "a2", "x3", "a3", "x0", "a4", "x5", "a5", "x2", "a6", "x7", "a7", "x4", "x6"]
 
 
 def pixel_runs(g):
@@ -36,7 +36,7 @@ def tile_windowattentionblock_pb_kernel(tc, attn_ctx, x, wo, bo, out):
 
     with ExitStack() as ctx:
         keep = ctx.enter_context(tc.tile_pool(name="keep", bufs=1))
-        work = ctx.enter_context(tc.tile_pool(name="work", bufs=4))
+        work = ctx.enter_context(tc.tile_pool(name="work", bufs=3))
         ybuf = ctx.enter_context(tc.tile_pool(name="ybuf", bufs=2))
         ps_a = ctx.enter_context(tc.psum_pool(name="ps_a", bufs=3))
         ps_b = ctx.enter_context(tc.psum_pool(name="ps_b", bufs=2))
@@ -97,8 +97,10 @@ def tile_windowattentionblock_pb_kernel(tc, attn_ctx, x, wo, bo, out):
         w_scales = keep.tile([P, 512], U8, name="w_scales", align_bytes=64)
         b_bc = keep.tile([P, 512], F32, name="b_bc")
 
-        def prepare_w():
+        def interleave_w():
             nc.vector.tensor_copy(out=w_grouped[:], in_=w_raw[:].rearrange("p j c -> p c j"))
+
+        def quantise_w():
             nc.vector.quantize_mx(
                 out=w_codes[:].bitcast(E4M3X4),
                 scales=w_scales[:],
@@ -118,8 +120,9 @@ def tile_windowattentionblock_pb_kernel(tc, attn_ctx, x, wo, bo, out):
             nc.scalar.copy(out=b_bc[:], in_=bb_ps[:])
 
         def add_bias_to_x(i):
-            for s in range(4):
-                nc.gpsimd.tensor_tensor(out=xb_sb[i][:, s, :], in0=x_sb[i][:, s, :], in1=b_bc[:], op=ADD)
+            nc.vector.tensor_tensor(
+                out=xb_sb[i][:], in0=x_sb[i][:], in1=b_bc[:].unsqueeze(1).to_broadcast([P, 4, 512]), op=ADD
+            )
 
         grouped = {}
         codes = {}
@@ -128,8 +131,9 @@ def tile_windowattentionblock_pb_kernel(tc, attn_ctx, x, wo, bo, out):
 
         def stage_a(i):
             words = a_sb[i][:].bitcast(F32)
-            grouped[i] = work.tile([P, 2048], BF16, name="grouped", align_bytes=64)
-            gw = grouped[i][:].bitcast(F32)
+            if i % 2 == 0:
+                grouped[i // 2] = work.tile([P, 4096], BF16, name="grouped", align_bytes=64)
+            gw = grouped[i // 2][:, 2048 * (i % 2) : 2048 * (i % 2 + 1)].bitcast(F32)
             for h in range(2):
                 xt = ps_a.tile([P, 2, 2, P], F32, name="xt")
                 for a in range(2):
@@ -143,12 +147,19 @@ def tile_windowattentionblock_pb_kernel(tc, attn_ctx, x, wo, bo, out):
                     in_=xt[:].rearrange("p a u q -> p a q u"),
                 )
 
-        def quantise(i):
-            codes[i] = work.tile([P, 512], U32, name="codes", align_bytes=64)
-            scales[i] = work.tile([P, 512], U8, name="scales", align_bytes=64)
-            nc.vector.quantize_mx(
-                out=codes[i][:].bitcast(E5M2X4), scales=scales[i][:], in_=grouped[i][:]
-            )
+        def quantise(j, parts):
+            pair_codes = work.tile([P, 1024], U32, name="codes", align_bytes=64)
+            pair_scales = work.tile([P, 1024], U8, name="scales", align_bytes=64)
+            for h in range(2):
+                codes[2 * j + h] = pair_codes[:, 512 * h : 512 * (h + 1)]
+                scales[2 * j + h] = pair_scales[:, 512 * h : 512 * (h + 1)]
+            width = 1024 // parts
+            for h in range(parts):
+                nc.vector.quantize_mx(
+                    out=pair_codes[:, width * h : width * (h + 1)].bitcast(E5M2X4),
+                    scales=pair_scales[:, width * h : width * (h + 1)],
+                    in_=grouped[j][:, 4 * width * h : 4 * width * (h + 1)],
+                )
 
         def store(i, s):
             for q0, q1, pix in pixel_runs(ORDER[i]):
@@ -170,7 +181,7 @@ def tile_windowattentionblock_pb_kernel(tc, attn_ctx, x, wo, bo, out):
                 start=True,
                 stop=True,
             )
-            nc.vector.tensor_tensor(out=o_sb[i][:, s, :], in0=xb_sb[i][:, s, :], in1=o_ps[:], op=ADD)
+            nc.vector.tensor_tensor(out=o_sb[i][:, s, :], in0=o_ps[:], in1=xb_sb[i][:, s, :], op=ADD)
             if fine:
                 store(i, s)
 
@@ -181,8 +192,8 @@ def tile_windowattentionblock_pb_kernel(tc, attn_ctx, x, wo, bo, out):
                 out=y_ps[:],
                 lhsT=w_codes[:, cols].bitcast(E4M3X4),
                 lhsT_scale=w_scales[:, cols],
-                rhs=codes[i][:].bitcast(E5M2X4),
-                rhs_scale=scales[i][:],
+                rhs=codes[i].bitcast(E5M2X4),
+                rhs_scale=scales[i],
                 start=True,
                 stop=True,
             )
@@ -197,20 +208,20 @@ def tile_windowattentionblock_pb_kernel(tc, attn_ctx, x, wo, bo, out):
                     nc.tensor.transpose(
                         o_ps[:, P * t : P * (t + 1)], y_sb[i][:, t, P * s : P * (s + 1)], ident[:]
                     )
-                nc.vector.tensor_tensor(out=o_sb[i][:, s, :], in0=x_sb[i][:, s, :], in1=o_ps[:], op=ADD)
+                nc.vector.tensor_tensor(out=o_sb[i][:, s, :], in0=o_ps[:], in1=x_sb[i][:, s, :], op=ADD)
                 if fine:
                     store(i, s)
             if not fine:
                 store(i, None)
 
-        stage_a(0)
         spread_bias()
+        interleave_w()
+        add_bias_to_x(1)
+        quantise_w()
+        stage_a(0)
         stage_a(1)
-        for i in range(1, BLOCKS, 2):
-            add_bias_to_x(i)
-        prepare_w()
-        quantise(0)
-        quantise(1)
+        quantise(0, 2)
+        add_bias_to_x(3)
         stage_a(2)
         stage_a(3)
         for j in range(PAIRS):
@@ -222,8 +233,9 @@ def tile_windowattentionblock_pb_kernel(tc, attn_ctx, x, wo, bo, out):
             if not fine:
                 store(2 * j + 1, None)
             if j + 1 < PAIRS:
-                quantise(2 * j + 2)
-                quantise(2 * j + 3)
+                quantise(j + 1, 1)
+            if j + 2 < PAIRS:
+                add_bias_to_x(2 * j + 5)
             if j + 2 < PAIRS:
                 stage_a(2 * j + 4)
                 stage_a(2 * j + 5)

@@ -23,8 +23,8 @@ LOADS = ["w", "x1", "a0", "a1", "a2", "x3", "a3", "x0", "a4", "x5", "a5", "x2", 
 
 def pixel_runs(g):
     if g < 7:
-        return [(0, 128, 512 * g + 256)]
-    return [(0, 64, 3840), (64, 128, 0)]
+        return [(slice(0, 128), 128, 512 * g + 256)]
+    return [(slice(0, 128, 2), 64, 3840), (slice(1, 128, 2), 64, 0)]
 
 
 def tile_windowattentionblock_pb_kernel(tc, attn_ctx, x, wo, bo, out):
@@ -70,10 +70,10 @@ def tile_windowattentionblock_pb_kernel(tc, attn_ctx, x, wo, bo, out):
                 )
             else:
                 i = int(what[1:])
-                for q0, q1, pix in pixel_runs(ORDER[i]):
+                for parts, count, pix in pixel_runs(ORDER[i]):
                     nc.sync.dma_start(
-                        out=x_sb[i][q0:q1, :, :],
-                        in_=x_rows[pix : pix + 4 * (q1 - q0), :].rearrange("(q s) c -> q s c", s=4),
+                        out=x_sb[i][parts, :, :],
+                        in_=x_rows[pix : pix + 4 * count, :].rearrange("(q s) c -> q s c", s=4),
                     )
 
         ident = keep.tile([P, P], F32, name="ident")
@@ -84,6 +84,13 @@ def tile_windowattentionblock_pb_kernel(tc, attn_ctx, x, wo, bo, out):
         nc.vector.tensor_copy(out=dst[:, :, :, 1], in_=src[:, :, :, 0])
         nc.vector.tensor_copy(out=dst[:, :, 1:8, 0], in_=src[:, :, 0:7, 1])
         nc.vector.tensor_copy(out=dst[:, :, 0, 0], in_=src[:, :, 7, 1])
+        perm_wrap = keep.tile([P, P], F32, name="perm_wrap")
+        src_w = ident[:].rearrange("p (a u t h) -> p u t a h", a=8, u=2, t=4, h=2)
+        dst_w = perm_wrap[:].rearrange("p (t a h u) -> p u t a h", t=4, a=8, h=2, u=2)
+        for u in range(2):
+            nc.vector.tensor_copy(out=dst_w[:, u, :, :, 1], in_=src_w[:, u, :, :, 0])
+            nc.vector.tensor_copy(out=dst_w[:, u, :, 1:8, 0], in_=src_w[:, u, :, 0:7, 1])
+            nc.vector.tensor_copy(out=dst_w[:, u, :, 0, 0], in_=src_w[:, u, :, 7, 1])
         ident_bf = keep.tile([P, P], BF16, name="ident_bf")
         nc.vector.tensor_copy(out=ident_bf[:], in_=ident[:])
 
@@ -140,7 +147,9 @@ def tile_windowattentionblock_pb_kernel(tc, attn_ctx, x, wo, bo, out):
                     s = 2 * h + a
                     for u in range(2):
                         nc.tensor.transpose(
-                            xt[:, a, u, :], words[:, 256 * s + u : 256 * (s + 1) : 2], perm[:]
+                            xt[:, a, u, :],
+                            words[:, 256 * s + u : 256 * (s + 1) : 2],
+                            perm_wrap[:] if ORDER[i] == 7 else perm[:],
                         )
                 nc.scalar.copy(
                     out=gw[:, 512 * h : 512 * (h + 1)].rearrange("p (a q u) -> p a q u", a=2, u=2),
@@ -162,12 +171,12 @@ def tile_windowattentionblock_pb_kernel(tc, attn_ctx, x, wo, bo, out):
                 )
 
         def store(i, s):
-            for q0, q1, pix in pixel_runs(ORDER[i]):
-                rows = o_rows[pix : pix + 4 * (q1 - q0), :].rearrange("(q s) c -> q s c", s=4)
+            for parts, count, pix in pixel_runs(ORDER[i]):
+                rows = o_rows[pix : pix + 4 * count, :].rearrange("(q s) c -> q s c", s=4)
                 if s is None:
-                    nc.sync.dma_start(out=rows, in_=o_sb[i][q0:q1, :, :])
+                    nc.sync.dma_start(out=rows, in_=o_sb[i][parts, :, :])
                 else:
-                    nc.sync.dma_start(out=rows[:, s, :], in_=o_sb[i][q0:q1, s, :])
+                    nc.sync.dma_start(out=rows[:, s, :], in_=o_sb[i][parts, s, :])
 
         def tokens_stationary(i, s, fine):
             cols = slice(P * s, P * (s + 1))

@@ -213,11 +213,24 @@ def tile_windowattentionblock_pb_kernel(tc, attn_ctx, x, wo, bo, out):
         def turn_back(i, fine):
             for s in range(4):
                 o_ps = ps_c.tile([P, 512], F32, name="o_ps")
-                for t in range(4):
-                    nc.tensor.transpose(
-                        o_ps[:, P * t : P * (t + 1)], y_sb[i][:, t, P * s : P * (s + 1)], ident[:]
-                    )
-                nc.vector.tensor_tensor(out=o_sb[i][:, s, :], in0=o_ps[:], in1=x_sb[i][:, s, :], op=ADD)
+                if s % 2 == 0:
+                    nc.tensor.matmul(out=o_ps[:], lhsT=ident_bf[:], rhs=x_sb[i][:, s, :], start=True, stop=False)
+                    for t in range(4):
+                        nc.tensor.matmul(
+                            out=o_ps[:, P * t : P * (t + 1)],
+                            lhsT=y_sb[i][:, t, P * s : P * (s + 1)],
+                            rhs=ident[:],
+                            is_transpose=True,
+                            start=False,
+                            stop=(t == 3),
+                        )
+                    nc.scalar.copy(out=o_sb[i][:, s, :], in_=o_ps[:])
+                else:
+                    for t in range(4):
+                        nc.tensor.transpose(
+                            o_ps[:, P * t : P * (t + 1)], y_sb[i][:, t, P * s : P * (s + 1)], ident[:]
+                        )
+                    nc.vector.tensor_tensor(out=o_sb[i][:, s, :], in0=o_ps[:], in1=x_sb[i][:, s, :], op=ADD)
                 if fine:
                     store(i, s)
             if not fine:

@@ -15,16 +15,20 @@ ADD = mybir.AluOpType.add
 IDENTITY = mybir.ActivationFunctionType.Identity
 
 P = 128
-BLOCKS = 8
-PAIRS = 4
+STRIPS = 8
 ORDER = [7, 0, 1, 2, 3, 4, 5, 6]
-LOADS = ["w", "x1", "a0", "a1", "a2", "x3", "a3", "x0", "a4", "x5", "a5", "x2", "a6", "x7", "a7", "x4", "x6"]
+LOADS = ["w", "a0", "x1", "a1", "a2", "x3", "a3", "x0", "a4", "x5", "a5", "x2", "a6", "x7", "a7", "x4", "x6"]
+AHEAD = 4
 
 
 def pixel_runs(g):
     if g < 7:
         return [(slice(0, 128), 128, 512 * g + 256)]
     return [(slice(0, 128, 2), 64, 3840), (slice(1, 128, 2), 64, 0)]
+
+
+def tokens_stationary(i):
+    return i % 2 == 1
 
 
 def tile_windowattentionblock_pb_kernel(tc, attn_ctx, x, wo, bo, out):
@@ -36,22 +40,20 @@ def tile_windowattentionblock_pb_kernel(tc, attn_ctx, x, wo, bo, out):
 
     with ExitStack() as ctx:
         keep = ctx.enter_context(tc.tile_pool(name="keep", bufs=1))
-        work = ctx.enter_context(tc.tile_pool(name="work", bufs=3))
+        work = ctx.enter_context(tc.tile_pool(name="work", bufs=4))
         ybuf = ctx.enter_context(tc.tile_pool(name="ybuf", bufs=2))
-        ps_a = ctx.enter_context(tc.psum_pool(name="ps_a", bufs=3))
-        ps_b = ctx.enter_context(tc.psum_pool(name="ps_b", bufs=2))
-        ps_c = ctx.enter_context(tc.psum_pool(name="ps_c", bufs=3))
+        psum = ctx.enter_context(tc.psum_pool(name="psum", bufs=8))
         ctx.enter_context(tc.manual_schedule())
 
         a_sb = {}
         x_sb = {}
         o_sb = {}
         xb_sb = {}
-        for i in range(BLOCKS):
+        for i in range(STRIPS):
             a_sb[i] = keep.tile([P, 2048], BF16, name="a_sb%d" % i)
             x_sb[i] = keep.tile([P, 4, 512], BF16, name="x_sb%d" % i)
             o_sb[i] = keep.tile([P, 4, 512], F32, name="o_sb%d" % i)
-            if i % 2 == 1:
+            if tokens_stationary(i):
                 xb_sb[i] = keep.tile([P, 4, 512], F32, name="xb_sb%d" % i)
         w_raw = keep.tile([P, 4, 512], BF16, name="w_raw")
         b_col = keep.tile([P, 4], BF16, name="b_col")
@@ -81,9 +83,6 @@ def tile_windowattentionblock_pb_kernel(tc, attn_ctx, x, wo, bo, out):
         perm = keep.tile([P, P], F32, name="perm")
         src = ident[:].rearrange("p (a t h) -> p t a h", a=8, t=8, h=2)
         dst = perm[:].rearrange("p (t a h) -> p t a h", t=8, a=8, h=2)
-        nc.vector.tensor_copy(out=dst[:, :, :, 1], in_=src[:, :, :, 0])
-        nc.vector.tensor_copy(out=dst[:, :, 1:8, 0], in_=src[:, :, 0:7, 1])
-        nc.vector.tensor_copy(out=dst[:, :, 0, 0], in_=src[:, :, 7, 1])
         perm_wrap = keep.tile([P, P], F32, name="perm_wrap")
         src_w = ident[:].rearrange("p (a u t h) -> p u t a h", a=8, u=2, t=4, h=2)
         dst_w = perm_wrap[:].rearrange("p (t a h u) -> p u t a h", t=4, a=8, h=2, u=2)
@@ -91,6 +90,9 @@ def tile_windowattentionblock_pb_kernel(tc, attn_ctx, x, wo, bo, out):
             nc.vector.tensor_copy(out=dst_w[:, u, :, :, 1], in_=src_w[:, u, :, :, 0])
             nc.vector.tensor_copy(out=dst_w[:, u, :, 1:8, 0], in_=src_w[:, u, :, 0:7, 1])
             nc.vector.tensor_copy(out=dst_w[:, u, :, 0, 0], in_=src_w[:, u, :, 7, 1])
+        nc.vector.tensor_copy(out=dst[:, :, :, 1], in_=src[:, :, :, 0])
+        nc.vector.tensor_copy(out=dst[:, :, 1:8, 0], in_=src[:, :, 0:7, 1])
+        nc.vector.tensor_copy(out=dst[:, :, 0, 0], in_=src[:, :, 7, 1])
         ident_bf = keep.tile([P, P], BF16, name="ident_bf")
         nc.vector.tensor_copy(out=ident_bf[:], in_=ident[:])
 
@@ -115,7 +117,7 @@ def tile_windowattentionblock_pb_kernel(tc, attn_ctx, x, wo, bo, out):
             )
 
         def spread_bias():
-            bb_ps = ps_c.tile([P, 512], F32, name="o_ps")
+            bb_ps = psum.tile([P, 512], F32, name="bank")
             for t in range(4):
                 nc.tensor.matmul(
                     out=bb_ps[:, P * t : P * (t + 1)],
@@ -136,129 +138,115 @@ def tile_windowattentionblock_pb_kernel(tc, attn_ctx, x, wo, bo, out):
         scales = {}
         y_sb = {}
 
-        def stage_a(i):
+        def first_transposes(bank):
+            i, h = divmod(bank, 2)
             words = a_sb[i][:].bitcast(F32)
-            if i % 2 == 0:
-                grouped[i // 2] = work.tile([P, 4096], BF16, name="grouped", align_bytes=64)
-            gw = grouped[i // 2][:, 2048 * (i % 2) : 2048 * (i % 2 + 1)].bitcast(F32)
-            for h in range(2):
-                xt = ps_a.tile([P, 2, 2, P], F32, name="xt")
-                for a in range(2):
-                    s = 2 * h + a
-                    for u in range(2):
-                        nc.tensor.transpose(
-                            xt[:, a, u, :],
-                            words[:, 256 * s + u : 256 * (s + 1) : 2],
-                            perm_wrap[:] if ORDER[i] == 7 else perm[:],
-                        )
-                nc.scalar.copy(
-                    out=gw[:, 512 * h : 512 * (h + 1)].rearrange("p (a q u) -> p a q u", a=2, u=2),
-                    in_=xt[:].rearrange("p a u q -> p a q u"),
-                )
+            if h == 0:
+                grouped[i] = work.tile([P, 2048], BF16, name="grouped", align_bytes=64)
+            xt = psum.tile([P, 2, 2, P], F32, name="bank")
+            for a in range(2):
+                s = 2 * h + a
+                for u in range(2):
+                    nc.tensor.transpose(
+                        xt[:, a, u, :],
+                        words[:, 256 * s + u : 256 * (s + 1) : 2],
+                        perm_wrap[:] if ORDER[i] == 7 else perm[:],
+                    )
+            nc.scalar.copy(
+                out=grouped[i][:, 1024 * h : 1024 * (h + 1)].bitcast(F32).rearrange("p (a q u) -> p a q u", a=2, u=2),
+                in_=xt[:].rearrange("p a u q -> p a q u"),
+            )
 
-        def quantise(j, parts):
-            pair_codes = work.tile([P, 1024], U32, name="codes", align_bytes=64)
-            pair_scales = work.tile([P, 1024], U8, name="scales", align_bytes=64)
-            for h in range(2):
-                codes[2 * j + h] = pair_codes[:, 512 * h : 512 * (h + 1)]
-                scales[2 * j + h] = pair_scales[:, 512 * h : 512 * (h + 1)]
-            width = 1024 // parts
-            for h in range(parts):
-                nc.vector.quantize_mx(
-                    out=pair_codes[:, width * h : width * (h + 1)].bitcast(E5M2X4),
-                    scales=pair_scales[:, width * h : width * (h + 1)],
-                    in_=grouped[j][:, 4 * width * h : 4 * width * (h + 1)],
-                )
+        def quantise(i):
+            codes[i] = work.tile([P, 512], U32, name="codes", align_bytes=64)
+            scales[i] = work.tile([P, 512], U8, name="scales", align_bytes=64)
+            nc.vector.quantize_mx(out=codes[i][:].bitcast(E5M2X4), scales=scales[i][:], in_=grouped[i][:])
 
-        def store(i, s):
+        def finished(i, s):
+            if i >= STRIPS - 2:
+                first = s
+            elif s % 2 == 1:
+                first = s - 1
+            else:
+                return
             for parts, count, pix in pixel_runs(ORDER[i]):
                 rows = o_rows[pix : pix + 4 * count, :].rearrange("(q s) c -> q s c", s=4)
-                if s is None:
-                    nc.sync.dma_start(out=rows, in_=o_sb[i][parts, :, :])
-                else:
-                    nc.sync.dma_start(out=rows[:, s, :], in_=o_sb[i][parts, s, :])
+                nc.sync.dma_start(out=rows[:, first : s + 1, :], in_=o_sb[i][parts, first : s + 1, :])
 
-        def tokens_stationary(i, s, fine):
-            cols = slice(P * s, P * (s + 1))
-            o_ps = ps_c.tile([P, 512], F32, name="o_ps")
-            nc.tensor.matmul_mx(
-                out=o_ps[:],
-                lhsT=codes[i][:, cols].bitcast(E5M2X4),
-                lhsT_scale=scales[i][:, cols],
-                rhs=w_codes[:].bitcast(E4M3X4),
-                rhs_scale=w_scales[:],
-                start=True,
-                stop=True,
-            )
-            nc.vector.tensor_tensor(out=o_sb[i][:, s, :], in0=o_ps[:], in1=xb_sb[i][:, s, :], op=ADD)
-            if fine:
-                store(i, s)
+        def product(i, r):
+            cols = slice(P * r, P * (r + 1))
+            bank = psum.tile([P, 512], F32, name="bank")
+            if tokens_stationary(i):
+                nc.tensor.matmul_mx(
+                    out=bank[:],
+                    lhsT=codes[i][:, cols].bitcast(E5M2X4),
+                    lhsT_scale=scales[i][:, cols],
+                    rhs=w_codes[:].bitcast(E4M3X4),
+                    rhs_scale=w_scales[:],
+                    start=True,
+                    stop=True,
+                )
+                nc.vector.tensor_tensor(out=o_sb[i][:, r, :], in0=bank[:], in1=xb_sb[i][:, r, :], op=ADD)
+                finished(i, r)
+            else:
+                if r == 0:
+                    y_sb[i] = ybuf.tile([P, 4, 512], F32, name="y_sb")
+                nc.tensor.matmul_mx(
+                    out=bank[:],
+                    lhsT=w_codes[:, cols].bitcast(E4M3X4),
+                    lhsT_scale=w_scales[:, cols],
+                    rhs=codes[i][:].bitcast(E5M2X4),
+                    rhs_scale=scales[i][:],
+                    start=True,
+                    stop=True,
+                )
+                nc.scalar.activation(
+                    out=y_sb[i][:, r, :], in_=bank[:], func=IDENTITY, bias=b_col[:, r : r + 1], scale=1.0
+                )
 
-        def weights_stationary(i, t):
-            cols = slice(P * t, P * (t + 1))
-            y_ps = ps_b.tile([P, 512], F32, name="y_ps")
-            nc.tensor.matmul_mx(
-                out=y_ps[:],
-                lhsT=w_codes[:, cols].bitcast(E4M3X4),
-                lhsT_scale=w_scales[:, cols],
-                rhs=codes[i].bitcast(E5M2X4),
-                rhs_scale=scales[i],
-                start=True,
-                stop=True,
-            )
-            nc.scalar.activation(
-                out=y_sb[i][:, t, :], in_=y_ps[:], func=IDENTITY, bias=b_col[:, t : t + 1], scale=1.0
-            )
-
-        def turn_back(i, fine):
-            for s in range(4):
-                o_ps = ps_c.tile([P, 512], F32, name="o_ps")
-                if s % 2 == 0:
-                    nc.tensor.matmul(out=o_ps[:], lhsT=ident_bf[:], rhs=x_sb[i][:, s, :], start=True, stop=False)
-                    for t in range(4):
-                        nc.tensor.matmul(
-                            out=o_ps[:, P * t : P * (t + 1)],
-                            lhsT=y_sb[i][:, t, P * s : P * (s + 1)],
-                            rhs=ident[:],
-                            is_transpose=True,
-                            start=False,
-                            stop=(t == 3),
-                        )
-                    nc.scalar.copy(out=o_sb[i][:, s, :], in_=o_ps[:])
-                else:
-                    for t in range(4):
-                        nc.tensor.transpose(
-                            o_ps[:, P * t : P * (t + 1)], y_sb[i][:, t, P * s : P * (s + 1)], ident[:]
-                        )
-                    nc.vector.tensor_tensor(out=o_sb[i][:, s, :], in0=o_ps[:], in1=x_sb[i][:, s, :], op=ADD)
-                if fine:
-                    store(i, s)
-            if not fine:
-                store(i, None)
+        def turn_back(i, s):
+            bank = psum.tile([P, 512], F32, name="bank")
+            if s % 2 == 0:
+                nc.tensor.matmul(out=bank[:], lhsT=ident_bf[:], rhs=x_sb[i][:, s, :], start=True, stop=False)
+                for t in range(4):
+                    nc.tensor.matmul(
+                        out=bank[:, P * t : P * (t + 1)],
+                        lhsT=y_sb[i][:, t, P * s : P * (s + 1)],
+                        rhs=ident[:],
+                        is_transpose=True,
+                        start=False,
+                        stop=(t == 3),
+                    )
+                nc.scalar.copy(out=o_sb[i][:, s, :], in_=bank[:])
+            else:
+                for t in range(4):
+                    nc.tensor.transpose(bank[:, P * t : P * (t + 1)], y_sb[i][:, t, P * s : P * (s + 1)], ident[:])
+                nc.vector.tensor_tensor(out=o_sb[i][:, s, :], in0=bank[:], in1=x_sb[i][:, s, :], op=ADD)
+            finished(i, s)
 
         spread_bias()
         interleave_w()
-        add_bias_to_x(1)
         quantise_w()
-        stage_a(0)
-        stage_a(1)
-        quantise(0, 2)
-        add_bias_to_x(3)
-        stage_a(2)
-        stage_a(3)
-        for j in range(PAIRS):
-            fine = j == PAIRS - 1
-            y_sb[2 * j] = ybuf.tile([P, 4, 512], F32, name="y_sb")
-            for r in range(4):
-                tokens_stationary(2 * j + 1, r, fine)
-                weights_stationary(2 * j, r)
-            if not fine:
-                store(2 * j + 1, None)
-            if j + 1 < PAIRS:
-                quantise(j + 1, 1)
-            if j + 2 < PAIRS:
-                add_bias_to_x(2 * j + 5)
-            if j + 2 < PAIRS:
-                stage_a(2 * j + 4)
-                stage_a(2 * j + 5)
-            turn_back(2 * j, fine)
+        for bank in range(AHEAD):
+            first_transposes(bank)
+        add_bias_to_x(1)
+        quantise(0)
+        to_turn = []
+        turned = 0
+        for period in range(2 * STRIPS):
+            i, half = divmod(period, 2)
+            product(i, 2 * half)
+            product(i, 2 * half + 1)
+            for n in range(2 if period >= 2 * STRIPS - 2 else 1):
+                if turned < len(to_turn):
+                    turn_back(to_turn[turned][0], to_turn[turned][1])
+                    turned += 1
+            if half == 1 and not tokens_stationary(i):
+                to_turn.extend([(i, s) for s in range(4)])
+            if period + AHEAD < 2 * STRIPS:
+                first_transposes(period + AHEAD)
+            if half == 0 and i + 1 < STRIPS:
+                quantise(i + 1)
+            if half == 1 and tokens_stationary(i) and i + 2 < STRIPS:
+                add_bias_to_x(i + 2)
+        assert turned == len(to_turn)

@@ -17,7 +17,7 @@ IDENTITY = mybir.ActivationFunctionType.Identity
 P = 128
 STRIPS = 8
 ORDER = [7, 0, 1, 2, 3, 4, 5, 6]
-LOADS = ["w", "a0", "x1", "a1", "a2", "x3", "a3", "x0", "a4", "x5", "a5", "x2", "a6", "x7", "a7", "x4", "x6"]
+LOADS = ["a0", "w", "a1", "x1", "a2", "x0", "a3", "x3", "a4", "x2", "a5", "x5", "a6", "x4", "a7", "x7", "x6"]
 AHEAD = 4
 
 
@@ -66,10 +66,12 @@ def tile_windowattentionblock_pb_kernel(tc, attn_ctx, x, wo, bo, out):
             elif what.startswith("a"):
                 i = int(what[1:])
                 g = ORDER[i]
-                nc.sync.dma_start(
-                    out=a_sb[i][:],
-                    in_=a_rows[512 * g : 512 * (g + 1), :].rearrange("(p s) k -> p (s k)", s=4),
-                )
+                rows = a_rows[512 * g : 512 * (g + 1), :].rearrange("(p s) k -> p s k", s=4)
+                tiles = a_sb[i][:].rearrange("p (s k) -> p s k", s=4)
+                pieces = 2 if i == 0 else 1
+                for h in range(pieces):
+                    part = slice(4 // pieces * h, 4 // pieces * (h + 1))
+                    nc.sync.dma_start(out=tiles[:, part, :], in_=rows[:, part, :])
             else:
                 i = int(what[1:])
                 for parts, count, pix in pixel_runs(ORDER[i]):
@@ -128,9 +130,13 @@ def tile_windowattentionblock_pb_kernel(tc, attn_ctx, x, wo, bo, out):
                 )
             nc.scalar.copy(out=b_bc[:], in_=bb_ps[:])
 
-        def add_bias_to_x(i):
+        def add_bias_to_x(i, half):
+            tiles = slice(2 * half, 2 * half + 2)
             nc.vector.tensor_tensor(
-                out=xb_sb[i][:], in0=x_sb[i][:], in1=b_bc[:].unsqueeze(1).to_broadcast([P, 4, 512]), op=ADD
+                out=xb_sb[i][:, tiles, :],
+                in0=x_sb[i][:, tiles, :],
+                in1=b_bc[:].unsqueeze(1).to_broadcast([P, 2, 512]),
+                op=ADD,
             )
 
         grouped = {}
@@ -224,12 +230,11 @@ def tile_windowattentionblock_pb_kernel(tc, attn_ctx, x, wo, bo, out):
                 nc.vector.tensor_tensor(out=o_sb[i][:, s, :], in0=bank[:], in1=x_sb[i][:, s, :], op=ADD)
             finished(i, s)
 
-        spread_bias()
         interleave_w()
         quantise_w()
         for bank in range(AHEAD):
             first_transposes(bank)
-        add_bias_to_x(1)
+        spread_bias()
         quantise(0)
         to_turn = []
         turned = 0
@@ -247,6 +252,6 @@ def tile_windowattentionblock_pb_kernel(tc, attn_ctx, x, wo, bo, out):
                 first_transposes(period + AHEAD)
             if half == 0 and i + 1 < STRIPS:
                 quantise(i + 1)
-            if half == 1 and tokens_stationary(i) and i + 2 < STRIPS:
-                add_bias_to_x(i + 2)
+            if not tokens_stationary(i):
+                add_bias_to_x(i + 1, half)
         assert turned == len(to_turn)

@@ -58,8 +58,9 @@ def tile_windowattentionblock_pb_kernel(tc, attn_ctx, x, wo, bo, out):
         w_raw = keep.tile([P, 4, 512], BF16, name="w_raw")
         b_col = keep.tile([P, 4], BF16, name="b_col")
 
-        with nc.allow_non_contiguous_dma(reason="512 bias values, one to a partition"):
-            nc.scalar.dma_start(out=b_col[:], in_=bo.rearrange("(t p) -> p t", p=P))
+        b_rows = keep.tile([P, P], BF16, name="b_rows")
+        nc.gpsimd.memset(b_rows[:], 0.0)
+        nc.scalar.dma_start(out=b_rows[0:4, :], in_=bo.rearrange("(t c) -> t c", t=4))
         for what in LOADS:
             if what == "w":
                 nc.sync.dma_start(out=w_raw[:], in_=w_rows.rearrange("(p j) c -> p j c", j=4))
@@ -117,6 +118,11 @@ def tile_windowattentionblock_pb_kernel(tc, attn_ctx, x, wo, bo, out):
                 scales=w_scales[:],
                 in_=w_grouped[:].rearrange("p c j -> p (c j)"),
             )
+
+        def bias_to_partitions():
+            bt_ps = psum.tile([P, P], BF16, name="bank")
+            nc.tensor.transpose(bt_ps[:], b_rows[:], ident_bf[:])
+            nc.scalar.copy(out=b_col[:], in_=bt_ps[:, 0:4])
 
         def spread_bias():
             bb_ps = psum.tile([P, 512], F32, name="bank")
@@ -230,6 +236,7 @@ def tile_windowattentionblock_pb_kernel(tc, attn_ctx, x, wo, bo, out):
                 nc.vector.tensor_tensor(out=o_sb[i][:, s, :], in0=bank[:], in1=x_sb[i][:, s, :], op=ADD)
             finished(i, s)
 
+        bias_to_partitions()
         interleave_w()
         quantise_w()
         for bank in range(AHEAD):

@@ -125,14 +125,10 @@ def tile_windowattentionblock_pb_kernel(tc, attn_ctx, x, wo, bo, out):
             nc.scalar.copy(out=b_col[:], in_=bt_ps[:, 0:4])
 
         def spread_bias():
-            bb_ps = psum.tile([P, 512], F32, name="bank")
+            bb_ps = psum.tile([P, 512], BF16, name="bank")
             for t in range(4):
-                nc.tensor.matmul(
-                    out=bb_ps[:, P * t : P * (t + 1)],
-                    lhsT=b_col[:, t : t + 1].to_broadcast([P, P]),
-                    rhs=ident_bf[:],
-                    start=True,
-                    stop=True,
+                nc.tensor.transpose(
+                    bb_ps[:, P * t : P * (t + 1)], b_col[:, t : t + 1].to_broadcast([P, P]), ident_bf[:]
                 )
             nc.scalar.copy(out=b_bc[:], in_=bb_ps[:])
 
@@ -218,7 +214,7 @@ def tile_windowattentionblock_pb_kernel(tc, attn_ctx, x, wo, bo, out):
 
         def turn_back(i, s):
             bank = psum.tile([P, 512], F32, name="bank")
-            if s % 2 == 0:
+            if s != 1:
                 nc.tensor.matmul(out=bank[:], lhsT=ident_bf[:], rhs=x_sb[i][:, s, :], start=True, stop=False)
                 for t in range(4):
                     nc.tensor.matmul(
@@ -236,12 +232,14 @@ def tile_windowattentionblock_pb_kernel(tc, attn_ctx, x, wo, bo, out):
                 nc.vector.tensor_tensor(out=o_sb[i][:, s, :], in0=bank[:], in1=x_sb[i][:, s, :], op=ADD)
             finished(i, s)
 
-        bias_to_partitions()
         interleave_w()
         quantise_w()
-        for bank in range(AHEAD):
-            first_transposes(bank)
+        first_transposes(0)
+        first_transposes(1)
+        bias_to_partitions()
         spread_bias()
+        for bank in range(2, AHEAD):
+            first_transposes(bank)
         quantise(0)
         to_turn = []
         turned = 0

@@ -58,6 +58,8 @@ def tile_windowattentionblock_pb_kernel(tc, attn_ctx, x, wo, bo, out):
         w_raw = keep.tile([P, 4, 512], BF16, name="w_raw")
         b_col = keep.tile([P, 4], BF16, name="b_col")
 
+        zeros = keep.tile([P, P], F32, name="zeros")
+        nc.gpsimd.memset(zeros[:], 0.0)
         b_rows = keep.tile([P, P], BF16, name="b_rows")
         nc.gpsimd.memset(b_rows[:], 0.0)
         nc.scalar.dma_start(out=b_rows[0:4, :], in_=bo.rearrange("(t c) -> t c", t=4))
@@ -109,15 +111,22 @@ def tile_windowattentionblock_pb_kernel(tc, attn_ctx, x, wo, bo, out):
         w_scales = keep.tile([P, 512], U8, name="w_scales", align_bytes=64)
         b_bc = keep.tile([P, 512], F32, name="b_bc")
 
-        def interleave_w():
-            nc.vector.tensor_copy(out=w_grouped[:], in_=w_raw[:].rearrange("p j c -> p c j"))
+        def interleave_w(t):
+            cols = slice(P * t, P * (t + 1))
+            nc.vector.tensor_copy(out=w_grouped[:, cols, :], in_=w_raw[:, :, cols].rearrange("p j c -> p c j"))
 
-        def quantise_w():
+        def quantise_w(t):
+            cols = slice(P * t, P * (t + 1))
             nc.vector.quantize_mx(
-                out=w_codes[:].bitcast(E4M3X4),
-                scales=w_scales[:],
-                in_=w_grouped[:].rearrange("p c j -> p (c j)"),
+                out=w_codes[:, cols].bitcast(E4M3X4),
+                scales=w_scales[:, cols],
+                in_=w_grouped[:, cols, :].rearrange("p c j -> p (c j)"),
             )
+
+        def keep_clock_up(count):
+            idle = psum.tile([P, P], F32, name="bank")
+            for n in range(count):
+                nc.tensor.matmul(out=idle[:], lhsT=zeros[:], rhs=zeros[:], start=True, stop=True)
 
         def bias_to_partitions():
             bt_ps = psum.tile([P, P], BF16, name="bank")
@@ -214,7 +223,7 @@ def tile_windowattentionblock_pb_kernel(tc, attn_ctx, x, wo, bo, out):
 
         def turn_back(i, s):
             bank = psum.tile([P, 512], F32, name="bank")
-            if s != 1:
+            if s % 2 == 0:
                 nc.tensor.matmul(out=bank[:], lhsT=ident_bf[:], rhs=x_sb[i][:, s, :], start=True, stop=False)
                 for t in range(4):
                     nc.tensor.matmul(
@@ -232,15 +241,27 @@ def tile_windowattentionblock_pb_kernel(tc, attn_ctx, x, wo, bo, out):
                 nc.vector.tensor_tensor(out=o_sb[i][:, s, :], in0=bank[:], in1=x_sb[i][:, s, :], op=ADD)
             finished(i, s)
 
-        interleave_w()
-        quantise_w()
+        keep_clock_up(5)
+        interleave_w(0)
+        interleave_w(1)
+        quantise_w(0)
+        quantise_w(1)
         first_transposes(0)
+        keep_clock_up(1)
         first_transposes(1)
+        keep_clock_up(1)
         bias_to_partitions()
+        keep_clock_up(2)
         spread_bias()
-        for bank in range(2, AHEAD):
-            first_transposes(bank)
         quantise(0)
+        interleave_w(2)
+        interleave_w(3)
+        quantise_w(2)
+        quantise_w(3)
+        first_transposes(2)
+        keep_clock_up(1)
+        first_transposes(3)
+        keep_clock_up(2)
         to_turn = []
         turned = 0
         for period in range(2 * STRIPS):

@@ -17,7 +17,7 @@ IDENTITY = mybir.ActivationFunctionType.Identity
 P = 128
 STRIPS = 8
 ORDER = [7, 0, 1, 2, 3, 4, 5, 6]
-LOADS = ["a0", "w", "a1", "x1", "a2", "x0", "a3", "x3", "a4", "x2", "a5", "x5", "a6", "x4", "a7", "x7", "x6"]
+LOADS = ["a0", "w", "a1", "x1", "a23", "x0", "x23", "a45", "x45", "a67", "x67"]
 AHEAD = 4
 
 
@@ -46,26 +46,47 @@ def tile_windowattentionblock_pb_kernel(tc, attn_ctx, x, wo, bo, out):
         ctx.enter_context(tc.manual_schedule())
 
         a_sb = {}
+        a_pair = {}
+        x_pair = {}
         x_sb = {}
         o_sb = {}
         xb_sb = {}
         for i in range(STRIPS):
-            a_sb[i] = keep.tile([P, 2048], BF16, name="a_sb%d" % i)
-            x_sb[i] = keep.tile([P, 4, 512], BF16, name="x_sb%d" % i)
+            if i < 2:
+                a_sb[i] = keep.tile([P, 2048], BF16, name="a_sb%d" % i)
+                x_sb[i] = keep.tile([P, 4, 512], BF16, name="x_sb%d" % i)
+            elif i % 2 == 0:
+                a_pair[i] = keep.tile([P, 2, 2048], BF16, name="a_pair%d" % i)
+                x_pair[i] = keep.tile([P, 2, 4, 512], BF16, name="x_pair%d" % i)
+                for j in range(2):
+                    a_sb[i + j] = a_pair[i][:, j, :]
+                    x_sb[i + j] = x_pair[i][:, j, :, :]
             o_sb[i] = keep.tile([P, 4, 512], F32, name="o_sb%d" % i)
             if tokens_stationary(i):
                 xb_sb[i] = keep.tile([P, 4, 512], F32, name="xb_sb%d" % i)
         w_raw = keep.tile([P, 4, 512], BF16, name="w_raw")
         b_col = keep.tile([P, 4], BF16, name="b_col")
 
-        zeros = keep.tile([P, P], F32, name="zeros")
-        nc.gpsimd.memset(zeros[:], 0.0)
         b_rows = keep.tile([P, P], BF16, name="b_rows")
         nc.gpsimd.memset(b_rows[:], 0.0)
         nc.scalar.dma_start(out=b_rows[0:4, :], in_=bo.rearrange("(t c) -> t c", t=4))
         for what in LOADS:
             if what == "w":
                 nc.sync.dma_start(out=w_raw[:], in_=w_rows.rearrange("(p j) c -> p j c", j=4))
+            elif len(what) == 3:
+                i = int(what[1])
+                g = ORDER[i]
+                if what.startswith("a"):
+                    nc.sync.dma_start(
+                        out=a_pair[i][:],
+                        in_=a_rows[512 * g : 512 * (g + 2), :].rearrange("(j p s) k -> p j (s k)", j=2, s=4),
+                    )
+                else:
+                    pix = 512 * g + 256
+                    nc.sync.dma_start(
+                        out=x_pair[i][:].rearrange("q j s c -> q j (s c)"),
+                        in_=x_rows[pix : pix + 1024, :].rearrange("(j q s) c -> q j (s c)", j=2, s=4),
+                    )
             elif what.startswith("a"):
                 i = int(what[1:])
                 g = ORDER[i]
@@ -122,11 +143,6 @@ def tile_windowattentionblock_pb_kernel(tc, attn_ctx, x, wo, bo, out):
                 scales=w_scales[:, cols],
                 in_=w_grouped[:, cols, :].rearrange("p c j -> p (c j)"),
             )
-
-        def keep_clock_up(count):
-            idle = psum.tile([P, P], F32, name="bank")
-            for n in range(count):
-                nc.tensor.matmul(out=idle[:], lhsT=zeros[:], rhs=zeros[:], start=True, stop=True)
 
         def bias_to_partitions():
             bt_ps = psum.tile([P, P], BF16, name="bank")
@@ -223,7 +239,7 @@ def tile_windowattentionblock_pb_kernel(tc, attn_ctx, x, wo, bo, out):
 
         def turn_back(i, s):
             bank = psum.tile([P, 512], F32, name="bank")
-            if s % 2 == 0:
+            if s != 1:
                 nc.tensor.matmul(out=bank[:], lhsT=ident_bf[:], rhs=x_sb[i][:, s, :], start=True, stop=False)
                 for t in range(4):
                     nc.tensor.matmul(
@@ -241,17 +257,13 @@ def tile_windowattentionblock_pb_kernel(tc, attn_ctx, x, wo, bo, out):
                 nc.vector.tensor_tensor(out=o_sb[i][:, s, :], in0=bank[:], in1=x_sb[i][:, s, :], op=ADD)
             finished(i, s)
 
-        keep_clock_up(5)
         interleave_w(0)
         interleave_w(1)
         quantise_w(0)
         quantise_w(1)
         first_transposes(0)
-        keep_clock_up(1)
         first_transposes(1)
-        keep_clock_up(1)
         bias_to_partitions()
-        keep_clock_up(2)
         spread_bias()
         quantise(0)
         interleave_w(2)
@@ -259,9 +271,7 @@ def tile_windowattentionblock_pb_kernel(tc, attn_ctx, x, wo, bo, out):
         quantise_w(2)
         quantise_w(3)
         first_transposes(2)
-        keep_clock_up(1)
         first_transposes(3)
-        keep_clock_up(2)
         to_turn = []
         turned = 0
         for period in range(2 * STRIPS):

@@ -17,7 +17,6 @@ IDENTITY = mybir.ActivationFunctionType.Identity
 P = 128
 STRIPS = 8
 ORDER = [7, 0, 1, 2, 3, 4, 5, 6]
-LOADS = ["a0", "w", "a1", "x1", "a23", "x0", "x23", "a45", "x45", "a67", "x67"]
 AHEAD = 4
 
 
@@ -53,14 +52,17 @@ def tile_windowattentionblock_pb_kernel(tc, attn_ctx, x, wo, bo, out):
         xb_sb = {}
         for i in range(STRIPS):
             if i < 2:
-                a_sb[i] = keep.tile([P, 2048], BF16, name="a_sb%d" % i)
                 x_sb[i] = keep.tile([P, 4, 512], BF16, name="x_sb%d" % i)
             elif i % 2 == 0:
-                a_pair[i] = keep.tile([P, 2, 2048], BF16, name="a_pair%d" % i)
                 x_pair[i] = keep.tile([P, 2, 4, 512], BF16, name="x_pair%d" % i)
                 for j in range(2):
-                    a_sb[i + j] = a_pair[i][:, j, :]
                     x_sb[i + j] = x_pair[i][:, j, :, :]
+            if i < 4:
+                a_sb[i] = keep.tile([P, 2048], BF16, name="a_sb%d" % i)
+            elif i % 2 == 0:
+                a_pair[i] = keep.tile([P, 2, 2048], BF16, name="a_pair%d" % i)
+                for j in range(2):
+                    a_sb[i + j] = a_pair[i][:, j, :]
             o_sb[i] = keep.tile([P, 4, 512], F32, name="o_sb%d" % i)
             if tokens_stationary(i):
                 xb_sb[i] = keep.tile([P, 4, 512], F32, name="xb_sb%d" % i)
@@ -70,39 +72,46 @@ def tile_windowattentionblock_pb_kernel(tc, attn_ctx, x, wo, bo, out):
         b_rows = keep.tile([P, P], BF16, name="b_rows")
         nc.gpsimd.memset(b_rows[:], 0.0)
         nc.scalar.dma_start(out=b_rows[0:4, :], in_=bo.rearrange("(t c) -> t c", t=4))
-        for what in LOADS:
-            if what == "w":
-                nc.sync.dma_start(out=w_raw[:], in_=w_rows.rearrange("(p j) c -> p j c", j=4))
-            elif len(what) == 3:
-                i = int(what[1])
-                g = ORDER[i]
-                if what.startswith("a"):
-                    nc.sync.dma_start(
-                        out=a_pair[i][:],
-                        in_=a_rows[512 * g : 512 * (g + 2), :].rearrange("(j p s) k -> p j (s k)", j=2, s=4),
-                    )
-                else:
-                    pix = 512 * g + 256
-                    nc.sync.dma_start(
-                        out=x_pair[i][:].rearrange("q j s c -> q j (s c)"),
-                        in_=x_rows[pix : pix + 1024, :].rearrange("(j q s) c -> q j (s c)", j=2, s=4),
-                    )
-            elif what.startswith("a"):
-                i = int(what[1:])
-                g = ORDER[i]
-                rows = a_rows[512 * g : 512 * (g + 1), :].rearrange("(p s) k -> p s k", s=4)
-                tiles = a_sb[i][:].rearrange("p (s k) -> p s k", s=4)
-                pieces = 2 if i == 0 else 1
-                for h in range(pieces):
-                    part = slice(4 // pieces * h, 4 // pieces * (h + 1))
-                    nc.sync.dma_start(out=tiles[:, part, :], in_=rows[:, part, :])
-            else:
-                i = int(what[1:])
-                for parts, count, pix in pixel_runs(ORDER[i]):
-                    nc.sync.dma_start(
-                        out=x_sb[i][parts, :, :],
-                        in_=x_rows[pix : pix + 4 * count, :].rearrange("(q s) c -> q s c", s=4),
-                    )
+        def load_a(i, pieces):
+            rows = a_rows[512 * ORDER[i] : 512 * (ORDER[i] + 1), :].rearrange("(p s) k -> p s k", s=4)
+            tiles = a_sb[i][:].rearrange("p (s k) -> p s k", s=4)
+            for h in range(pieces):
+                part = slice(4 // pieces * h, 4 // pieces * (h + 1))
+                nc.sync.dma_start(out=tiles[:, part, :], in_=rows[:, part, :])
+
+        def load_a_pair(i):
+            g = ORDER[i]
+            nc.sync.dma_start(
+                out=a_pair[i][:],
+                in_=a_rows[512 * g : 512 * (g + 2), :].rearrange("(j p s) k -> p j (s k)", j=2, s=4),
+            )
+
+        def load_x(i):
+            for parts, count, pix in pixel_runs(ORDER[i]):
+                nc.sync.dma_start(
+                    out=x_sb[i][parts, :, :],
+                    in_=x_rows[pix : pix + 4 * count, :].rearrange("(q s) c -> q s c", s=4),
+                )
+
+        def load_x_pair(i):
+            pix = 512 * ORDER[i] + 256
+            nc.sync.dma_start(
+                out=x_pair[i][:].rearrange("q j s c -> q j (s c)"),
+                in_=x_rows[pix : pix + 1024, :].rearrange("(j q s) c -> q j (s c)", j=2, s=4),
+            )
+
+        load_a(0, 2)
+        nc.sync.dma_start(out=w_raw[:], in_=w_rows.rearrange("(p j) c -> p j c", j=4))
+        load_a(1, 1)
+        load_x(1)
+        load_a(2, 1)
+        load_x(0)
+        load_a(3, 1)
+        load_x_pair(2)
+        load_a_pair(4)
+        load_x_pair(4)
+        load_a_pair(6)
+        load_x_pair(6)
 
         ident = keep.tile([P, P], F32, name="ident")
         make_identity(nc, ident[:])
@@ -155,7 +164,7 @@ def tile_windowattentionblock_pb_kernel(tc, attn_ctx, x, wo, bo, out):
                 nc.tensor.transpose(
                     bb_ps[:, P * t : P * (t + 1)], b_col[:, t : t + 1].to_broadcast([P, P]), ident_bf[:]
                 )
-            nc.scalar.copy(out=b_bc[:], in_=bb_ps[:])
+            nc.vector.tensor_copy(out=b_bc[:], in_=bb_ps[:])
 
         def add_bias_to_x(i, half):
             tiles = slice(2 * half, 2 * half + 2)
@@ -264,13 +273,13 @@ def tile_windowattentionblock_pb_kernel(tc, attn_ctx, x, wo, bo, out):
         first_transposes(0)
         first_transposes(1)
         bias_to_partitions()
-        spread_bias()
+        first_transposes(2)
         quantise(0)
         interleave_w(2)
         interleave_w(3)
         quantise_w(2)
         quantise_w(3)
-        first_transposes(2)
+        spread_bias()
         first_transposes(3)
         to_turn = []
         turned = 0
@@ -278,14 +287,14 @@ def tile_windowattentionblock_pb_kernel(tc, attn_ctx, x, wo, bo, out):
             i, half = divmod(period, 2)
             product(i, 2 * half)
             product(i, 2 * half + 1)
+            if period + AHEAD < 2 * STRIPS:
+                first_transposes(period + AHEAD)
             for n in range(2 if period >= 2 * STRIPS - 2 else 1):
                 if turned < len(to_turn):
                     turn_back(to_turn[turned][0], to_turn[turned][1])
                     turned += 1
             if half == 1 and not tokens_stationary(i):
                 to_turn.extend([(i, s) for s in range(4)])
-            if period + AHEAD < 2 * STRIPS:
-                first_transposes(period + AHEAD)
             if half == 0 and i + 1 < STRIPS:
                 quantise(i + 1)
             if not tokens_stationary(i):

@@ -246,25 +246,30 @@ def tile_windowattentionblock_pb_kernel(tc, attn_ctx, x, wo, bo, out):
                     out=y_sb[i][:, r, :], in_=bank[:], func=IDENTITY, bias=b_col[:, r : r + 1], scale=1.0
                 )
 
-        def turn_back(i, s):
-            bank = psum.tile([P, 512], F32, name="bank")
-            if s != 1:
-                nc.tensor.matmul(out=bank[:], lhsT=ident_bf[:], rhs=x_sb[i][:, s, :], start=True, stop=False)
-                for t in range(4):
-                    nc.tensor.matmul(
-                        out=bank[:, P * t : P * (t + 1)],
-                        lhsT=y_sb[i][:, t, P * s : P * (s + 1)],
-                        rhs=ident[:],
-                        is_transpose=True,
-                        start=False,
-                        stop=(t == 3),
-                    )
-                nc.scalar.copy(out=o_sb[i][:, s, :], in_=bank[:])
-            else:
-                for t in range(4):
-                    nc.tensor.transpose(bank[:, P * t : P * (t + 1)], y_sb[i][:, t, P * s : P * (s + 1)], ident[:])
-                nc.vector.tensor_tensor(out=o_sb[i][:, s, :], in0=bank[:], in1=x_sb[i][:, s, :], op=ADD)
-            finished(i, s)
+        def turn_back(turns):
+            banks = []
+            for i, s in turns:
+                bank = psum.tile([P, 512], F32, name="bank")
+                banks.append(bank)
+                if s != 1:
+                    nc.tensor.matmul(out=bank[:], lhsT=ident_bf[:], rhs=x_sb[i][:, s, :], start=True, stop=False)
+            for (i, s), bank in zip(turns, banks):
+                if s != 1:
+                    for t in range(4):
+                        nc.tensor.matmul(
+                            out=bank[:, P * t : P * (t + 1)],
+                            lhsT=y_sb[i][:, t, P * s : P * (s + 1)],
+                            rhs=ident[:],
+                            is_transpose=True,
+                            start=False,
+                            stop=(t == 3),
+                        )
+                    nc.scalar.copy(out=o_sb[i][:, s, :], in_=bank[:])
+                else:
+                    for t in range(4):
+                        nc.tensor.transpose(bank[:, P * t : P * (t + 1)], y_sb[i][:, t, P * s : P * (s + 1)], ident[:])
+                    nc.vector.tensor_tensor(out=o_sb[i][:, s, :], in0=bank[:], in1=x_sb[i][:, s, :], op=ADD)
+                finished(i, s)
 
         interleave_w(0)
         interleave_w(1)
@@ -282,21 +287,20 @@ def tile_windowattentionblock_pb_kernel(tc, attn_ctx, x, wo, bo, out):
         spread_bias()
         first_transposes(3)
         to_turn = []
-        turned = 0
-        for period in range(2 * STRIPS):
-            i, half = divmod(period, 2)
-            product(i, 2 * half)
-            product(i, 2 * half + 1)
-            if period + AHEAD < 2 * STRIPS:
-                first_transposes(period + AHEAD)
-            for n in range(2 if period >= 2 * STRIPS - 2 else 1):
-                if turned < len(to_turn):
-                    turn_back(to_turn[turned][0], to_turn[turned][1])
-                    turned += 1
-            if half == 1 and not tokens_stationary(i):
-                to_turn.extend([(i, s) for s in range(4)])
-            if half == 0 and i + 1 < STRIPS:
-                quantise(i + 1)
+        for i in range(STRIPS):
+            for r in range(4):
+                product(i, r)
+                if r == 1 and i + 1 < STRIPS:
+                    quantise(i + 1)
+                    if not tokens_stationary(i):
+                        add_bias_to_x(i + 1, 0)
             if not tokens_stationary(i):
-                add_bias_to_x(i + 1, half)
-        assert turned == len(to_turn)
+                add_bias_to_x(i + 1, 1)
+            count = 2 if i + 1 < STRIPS else len(to_turn)
+            turn_back(to_turn[:count])
+            to_turn = to_turn[count:]
+            if not tokens_stationary(i):
+                to_turn.extend([(i, s) for s in range(4)])
+            for bank in range(2 * i + AHEAD, 2 * i + AHEAD + 2):
+                if bank < 2 * STRIPS:
+                    first_transposes(bank)

@@ -16,14 +16,9 @@ IDENTITY = mybir.ActivationFunctionType.Identity
 
 P = 128
 STRIPS = 8
-ORDER = [7, 0, 1, 2, 3, 4, 5, 6]
+ORDER = [0, 7, 1, 2, 3, 4, 5, 6]
+WRAP = 7
 AHEAD = 4
-
-
-def pixel_runs(g):
-    if g < 7:
-        return [(slice(0, 128), 128, 512 * g + 256)]
-    return [(slice(0, 128, 2), 64, 3840), (slice(1, 128, 2), 64, 0)]
 
 
 def tokens_stationary(i):
@@ -87,10 +82,15 @@ def tile_windowattentionblock_pb_kernel(tc, attn_ctx, x, wo, bo, out):
             )
 
         def load_x(i):
-            for parts, count, pix in pixel_runs(ORDER[i]):
+            if ORDER[i] == WRAP:
                 nc.sync.dma_start(
-                    out=x_sb[i][parts, :, :],
-                    in_=x_rows[pix : pix + 4 * count, :].rearrange("(q s) c -> q s c", s=4),
+                    out=x_sb[i][:].rearrange("q (r s) c -> q r (s c)", r=2),
+                    in_=x_rows.rearrange("(r q s) c -> q r (s c)", r=16, s=2)[:, 0:16:15, :],
+                )
+            else:
+                pix = 512 * ORDER[i] + 256
+                nc.sync.dma_start(
+                    out=x_sb[i][:], in_=x_rows[pix : pix + 512, :].rearrange("(q s) c -> q s c", s=4)
                 )
 
         def load_x_pair(i):
@@ -120,14 +120,14 @@ def tile_windowattentionblock_pb_kernel(tc, attn_ctx, x, wo, bo, out):
         dst = perm[:].rearrange("p (t a h) -> p t a h", t=8, a=8, h=2)
         perm_wrap = keep.tile([P, P], F32, name="perm_wrap")
         src_w = ident[:].rearrange("p (a u t h) -> p u t a h", a=8, u=2, t=4, h=2)
-        dst_w = perm_wrap[:].rearrange("p (t a h u) -> p u t a h", t=4, a=8, h=2, u=2)
-        for u in range(2):
-            nc.vector.tensor_copy(out=dst_w[:, u, :, :, 1], in_=src_w[:, u, :, :, 0])
-            nc.vector.tensor_copy(out=dst_w[:, u, :, 1:8, 0], in_=src_w[:, u, :, 0:7, 1])
-            nc.vector.tensor_copy(out=dst_w[:, u, :, 0, 0], in_=src_w[:, u, :, 7, 1])
+        dst_w = perm_wrap[:].rearrange("p (v t a h) -> p v t a h", v=2, t=4, a=8, h=2)
         nc.vector.tensor_copy(out=dst[:, :, :, 1], in_=src[:, :, :, 0])
         nc.vector.tensor_copy(out=dst[:, :, 1:8, 0], in_=src[:, :, 0:7, 1])
         nc.vector.tensor_copy(out=dst[:, :, 0, 0], in_=src[:, :, 7, 1])
+        for v in range(2):
+            nc.vector.tensor_copy(out=dst_w[:, v, :, :, 1], in_=src_w[:, 1 - v, :, :, 0])
+            nc.vector.tensor_copy(out=dst_w[:, v, :, 1:8, 0], in_=src_w[:, 1 - v, :, 0:7, 1])
+            nc.vector.tensor_copy(out=dst_w[:, v, :, 0, 0], in_=src_w[:, 1 - v, :, 7, 1])
         ident_bf = keep.tile([P, P], BF16, name="ident_bf")
         nc.vector.tensor_copy(out=ident_bf[:], in_=ident[:])
 
@@ -186,18 +186,29 @@ def tile_windowattentionblock_pb_kernel(tc, attn_ctx, x, wo, bo, out):
             if h == 0:
                 grouped[i] = work.tile([P, 2048], BF16, name="grouped", align_bytes=64)
             xt = psum.tile([P, 2, 2, P], F32, name="bank")
+            wrap = ORDER[i] == WRAP
             for a in range(2):
-                s = 2 * h + a
+                s = h + 2 * a if wrap else 2 * h + a
                 for u in range(2):
                     nc.tensor.transpose(
                         xt[:, a, u, :],
                         words[:, 256 * s + u : 256 * (s + 1) : 2],
-                        perm_wrap[:] if ORDER[i] == 7 else perm[:],
+                        perm_wrap[:] if wrap else perm[:],
                     )
-            nc.scalar.copy(
-                out=grouped[i][:, 1024 * h : 1024 * (h + 1)].bitcast(F32).rearrange("p (a q u) -> p a q u", a=2, u=2),
-                in_=xt[:].rearrange("p a u q -> p a q u"),
-            )
+            if wrap:
+                for v in range(2):
+                    first = 512 * (2 * v + h)
+                    nc.scalar.copy(
+                        out=grouped[i][:, first : first + 512].bitcast(F32).rearrange("p (m a u) -> p m a u", a=2, u=2),
+                        in_=xt[:, :, :, 64 * v : 64 * (v + 1)].rearrange("p a u m -> p m a u"),
+                    )
+            else:
+                nc.scalar.copy(
+                    out=grouped[i][:, 1024 * h : 1024 * (h + 1)]
+                    .bitcast(F32)
+                    .rearrange("p (a q u) -> p a q u", a=2, u=2),
+                    in_=xt[:].rearrange("p a u q -> p a q u"),
+                )
 
         def quantise(i):
             codes[i] = work.tile([P, 512], U32, name="codes", align_bytes=64)
@@ -211,9 +222,13 @@ def tile_windowattentionblock_pb_kernel(tc, attn_ctx, x, wo, bo, out):
                 first = s - 1
             else:
                 return
-            for parts, count, pix in pixel_runs(ORDER[i]):
-                rows = o_rows[pix : pix + 4 * count, :].rearrange("(q s) c -> q s c", s=4)
-                nc.sync.dma_start(out=rows[:, first : s + 1, :], in_=o_sb[i][parts, first : s + 1, :])
+            if ORDER[i] == WRAP:
+                pix = 0 if first == 0 else 3840
+                rows = o_rows[pix : pix + 256, :].rearrange("(q s) c -> q s c", s=2)
+            else:
+                pix = 512 * ORDER[i] + 256
+                rows = o_rows[pix : pix + 512, :].rearrange("(q s) c -> q s c", s=4)[:, first : s + 1, :]
+            nc.sync.dma_start(out=rows, in_=o_sb[i][:, first : s + 1, :])
 
         def product(i, r):
             cols = slice(P * r, P * (r + 1))

@@ -49,15 +49,15 @@ def tile_windowattentionblock_pb_kernel(tc, attn_ctx, x, wo, bo, out):
             if i < 2:
                 x_sb[i] = keep.tile([P, 4, 512], BF16, name="x_sb%d" % i)
             elif i % 2 == 0:
-                x_pair[i] = keep.tile([P, 2, 4, 512], BF16, name="x_pair%d" % i)
+                x_pair[i] = keep.tile([P, 8, 512], BF16, name="x_pair%d" % i)
                 for j in range(2):
-                    x_sb[i + j] = x_pair[i][:, j, :, :]
-            if i < 4:
+                    x_sb[i + j] = x_pair[i][:, 4 * (1 - j) : 4 * (2 - j), :]
+            if i < 2:
                 a_sb[i] = keep.tile([P, 2048], BF16, name="a_sb%d" % i)
             elif i % 2 == 0:
-                a_pair[i] = keep.tile([P, 2, 2048], BF16, name="a_pair%d" % i)
+                a_pair[i] = keep.tile([P, 4096], BF16, name="a_pair%d" % i)
                 for j in range(2):
-                    a_sb[i + j] = a_pair[i][:, j, :]
+                    a_sb[i + j] = a_pair[i][:, 2048 * j : 2048 * (j + 1)]
             o_sb[i] = keep.tile([P, 4, 512], F32, name="o_sb%d" % i)
             if tokens_stationary(i):
                 xb_sb[i] = keep.tile([P, 4, 512], F32, name="xb_sb%d" % i)
@@ -78,7 +78,7 @@ def tile_windowattentionblock_pb_kernel(tc, attn_ctx, x, wo, bo, out):
             g = ORDER[i]
             nc.sync.dma_start(
                 out=a_pair[i][:],
-                in_=a_rows[512 * g : 512 * (g + 2), :].rearrange("(j p s) k -> p j (s k)", j=2, s=4),
+                in_=a_rows[512 * g : 512 * (g + 2), :].rearrange("(p s) k -> p (s k)", s=8),
             )
 
         def load_x(i):
@@ -96,17 +96,16 @@ def tile_windowattentionblock_pb_kernel(tc, attn_ctx, x, wo, bo, out):
         def load_x_pair(i):
             pix = 512 * ORDER[i] + 256
             nc.sync.dma_start(
-                out=x_pair[i][:].rearrange("q j s c -> q j (s c)"),
-                in_=x_rows[pix : pix + 1024, :].rearrange("(j q s) c -> q j (s c)", j=2, s=4),
+                out=x_pair[i][:],
+                in_=x_rows[pix : pix + 1024, :].rearrange("(q s) c -> q s c", s=8),
             )
 
         load_a(0, 2)
         nc.sync.dma_start(out=w_raw[:], in_=w_rows.rearrange("(p j) c -> p j c", j=4))
         load_a(1, 1)
+        load_a_pair(2)
         load_x(1)
-        load_a(2, 1)
         load_x(0)
-        load_a(3, 1)
         load_x_pair(2)
         load_a_pair(4)
         load_x_pair(4)
@@ -128,6 +127,15 @@ def tile_windowattentionblock_pb_kernel(tc, attn_ctx, x, wo, bo, out):
             nc.vector.tensor_copy(out=dst_w[:, v, :, :, 1], in_=src_w[:, 1 - v, :, :, 0])
             nc.vector.tensor_copy(out=dst_w[:, v, :, 1:8, 0], in_=src_w[:, 1 - v, :, 0:7, 1])
             nc.vector.tensor_copy(out=dst_w[:, v, :, 0, 0], in_=src_w[:, 1 - v, :, 7, 1])
+        perm_pair = []
+        src_p = ident[:].rearrange("p (b a t) -> p b t a", b=2, a=8, t=8)
+        for j in range(2):
+            perm_j = keep.tile([P, P], F32, name="perm_pair%d" % j)
+            perm_pair.append(perm_j)
+            dst_p = perm_j[:].rearrange("p (b t a) -> p b t a", b=2, t=8, a=8)
+            nc.vector.tensor_copy(out=dst_p[:, :, :, j:8], in_=src_p[:, :, :, 0 : 8 - j])
+            if j == 1:
+                nc.vector.tensor_copy(out=dst_p[:, :, :, 0], in_=src_p[:, :, :, 7])
         ident_bf = keep.tile([P, P], BF16, name="ident_bf")
         nc.vector.tensor_copy(out=ident_bf[:], in_=ident[:])
 
@@ -187,13 +195,14 @@ def tile_windowattentionblock_pb_kernel(tc, attn_ctx, x, wo, bo, out):
                 grouped[i] = work.tile([P, 2048], BF16, name="grouped", align_bytes=64)
             xt = psum.tile([P, 2, 2, P], F32, name="bank")
             wrap = ORDER[i] == WRAP
+            order = perm if i == 0 else perm_wrap if i == 1 else perm_pair[i % 2]
             for a in range(2):
                 s = h + 2 * a if wrap else 2 * h + a
                 for u in range(2):
                     nc.tensor.transpose(
                         xt[:, a, u, :],
                         words[:, 256 * s + u : 256 * (s + 1) : 2],
-                        perm_wrap[:] if wrap else perm[:],
+                        order[:],
                     )
             if wrap:
                 for v in range(2):
@@ -227,7 +236,13 @@ def tile_windowattentionblock_pb_kernel(tc, attn_ctx, x, wo, bo, out):
                 rows = o_rows[pix : pix + 256, :].rearrange("(q s) c -> q s c", s=2)
             else:
                 pix = 512 * ORDER[i] + 256
-                rows = o_rows[pix : pix + 512, :].rearrange("(q s) c -> q s c", s=4)[:, first : s + 1, :]
+                if i == 0:
+                    rows = o_rows[pix : pix + 512, :].rearrange("(q s) c -> q s c", s=4)[:, first : s + 1, :]
+                else:
+                    pix = pix - 512 * (i % 2)
+                    slot = first + 4 * (1 - i % 2)
+                    rows = o_rows[pix : pix + 1024, :].rearrange("(q s) c -> q s c", s=8)
+                    rows = rows[:, slot : slot + s + 1 - first, :]
             nc.sync.dma_start(out=rows, in_=o_sb[i][:, first : s + 1, :])
 
         def product(i, r):

@@ -103,8 +103,8 @@ def tile_windowattentionblock_pb_kernel(tc, attn_ctx, x, wo, bo, out):
         load_a(0, 2)
         nc.sync.dma_start(out=w_raw[:], in_=w_rows.rearrange("(p j) c -> p j c", j=4))
         load_a(1, 1)
-        load_a_pair(2)
         load_x(1)
+        load_a_pair(2)
         load_x(0)
         load_x_pair(2)
         load_a_pair(4)
@@ -225,12 +225,16 @@ def tile_windowattentionblock_pb_kernel(tc, attn_ctx, x, wo, bo, out):
             nc.vector.quantize_mx(out=codes[i][:].bitcast(E5M2X4), scales=scales[i][:], in_=grouped[i][:])
 
         def finished(i, s):
-            if i >= STRIPS - 2:
-                first = s
-            elif s % 2 == 1:
-                first = s - 1
+            if i == STRIPS - 1:
+                pieces = 4
+            elif i == 1 or i >= STRIPS - 4:
+                pieces = 2
             else:
+                pieces = 1
+            tiles = 4 // pieces
+            if (s + 1) % tiles != 0:
                 return
+            first = s + 1 - tiles
             if ORDER[i] == WRAP:
                 pix = 0 if first == 0 else 3840
                 rows = o_rows[pix : pix + 256, :].rearrange("(q s) c -> q s c", s=2)
@@ -316,13 +320,14 @@ def tile_windowattentionblock_pb_kernel(tc, attn_ctx, x, wo, bo, out):
         quantise_w(3)
         spread_bias()
         first_transposes(3)
+        add_bias_to_x(1, 0)
         to_turn = []
         for i in range(STRIPS):
             for r in range(4):
                 product(i, r)
                 if r == 1 and i + 1 < STRIPS:
                     quantise(i + 1)
-                    if not tokens_stationary(i):
+                    if not tokens_stationary(i) and i > 0:
                         add_bias_to_x(i + 1, 0)
             if not tokens_stationary(i):
                 add_bias_to_x(i + 1, 1)

@@ -149,9 +149,9 @@ def tile_windowattentionblock_pb_kernel(tc, attn_ctx, x, wo, bo, out):
         w_scales = keep.tile([P, 512], U8, name="w_scales", align_bytes=64)
         b_bc = keep.tile([P, 512], F32, name="b_bc")
 
-        def interleave_w(t):
+        def interleave_w(t, copy):
             cols = slice(P * t, P * (t + 1))
-            nc.vector.tensor_copy(out=w_grouped[:, cols, :], in_=w_raw[:, :, cols].rearrange("p j c -> p c j"))
+            copy(out=w_grouped[:, cols, :], in_=w_raw[:, :, cols].rearrange("p j c -> p c j"))
 
         def quantise_w(t):
             cols = slice(P * t, P * (t + 1))
@@ -305,24 +305,27 @@ def tile_windowattentionblock_pb_kernel(tc, attn_ctx, x, wo, bo, out):
                     nc.vector.tensor_tensor(out=o_sb[i][:, s, :], in0=bank[:], in1=x_sb[i][:, s, :], op=ADD)
                 finished(i, s)
 
-        interleave_w(0)
-        interleave_w(1)
+        interleave_w(0, nc.vector.tensor_copy)
+        interleave_w(1, nc.vector.tensor_copy)
         quantise_w(0)
         quantise_w(1)
         first_transposes(0)
         first_transposes(1)
         bias_to_partitions()
-        first_transposes(2)
         quantise(0)
-        interleave_w(2)
-        interleave_w(3)
+        spread_bias()
+        interleave_w(2, nc.scalar.copy)
+        interleave_w(3, nc.scalar.copy)
+        first_transposes(2)
+        first_transposes(3)
         quantise_w(2)
         quantise_w(3)
-        spread_bias()
-        first_transposes(3)
         add_bias_to_x(1, 0)
         to_turn = []
         for i in range(STRIPS):
+            if i == STRIPS - 2:
+                turn_back(to_turn)
+                to_turn = []
             for r in range(4):
                 product(i, r)
                 if r == 1 and i + 1 < STRIPS:

from contextlib import ExitStack

import concourse.mybir as mybir
from concourse.masks import make_identity

FLOPS = 2 * 4096 * 512 * 512

F32 = mybir.dt.float32
BF16 = mybir.dt.bfloat16
U32 = mybir.dt.uint32
U8 = mybir.dt.uint8
E5M2X4 = mybir.dt.float8_e5m2_x4
E4M3X4 = mybir.dt.float8_e4m3fn_x4
ADD = mybir.AluOpType.add
IDENTITY = mybir.ActivationFunctionType.Identity

P = 128
STRIPS = 8
ORDER = [0, 7, 1, 2, 3, 4, 5, 6]
WRAP = 7
AHEAD = 4


def tokens_stationary(i):
    return i % 2 == 1


def tile_windowattentionblock_pb_kernel(tc, attn_ctx, x, wo, bo, out):
    nc = tc.nc
    a_rows = attn_ctx.rearrange("n t h d -> (n t) (h d)")
    x_rows = x.rearrange("b i j c -> (b i j) c")
    o_rows = out.rearrange("b i j c -> (b i j) c")
    w_rows = wo.rearrange("h d c -> (h d) c")

    with ExitStack() as ctx:
        keep = ctx.enter_context(tc.tile_pool(name="keep", bufs=1))
        work = ctx.enter_context(tc.tile_pool(name="work", bufs=4))
        ybuf = ctx.enter_context(tc.tile_pool(name="ybuf", bufs=2))
        psum = ctx.enter_context(tc.psum_pool(name="psum", bufs=8))
        ctx.enter_context(tc.manual_schedule())

        a_sb = {}
        a_pair = {}
        x_pair = {}
        x_sb = {}
        o_sb = {}
        xb_sb = {}
        for i in range(STRIPS):
            if i < 2:
                x_sb[i] = keep.tile([P, 4, 512], BF16, name="x_sb%d" % i)
            elif i % 2 == 0:
                x_pair[i] = keep.tile([P, 8, 512], BF16, name="x_pair%d" % i)
                for j in range(2):
                    x_sb[i + j] = x_pair[i][:, 4 * (1 - j) : 4 * (2 - j), :]
            if i < 2:
                a_sb[i] = keep.tile([P, 2048], BF16, name="a_sb%d" % i)
            elif i % 2 == 0:
                a_pair[i] = keep.tile([P, 4096], BF16, name="a_pair%d" % i)
                for j in range(2):
                    a_sb[i + j] = a_pair[i][:, 2048 * j : 2048 * (j + 1)]
            o_sb[i] = keep.tile([P, 4, 512], F32, name="o_sb%d" % i)
            if tokens_stationary(i):
                xb_sb[i] = keep.tile([P, 4, 512], F32, name="xb_sb%d" % i)
        w_raw = keep.tile([P, 4, 512], BF16, name="w_raw")
        b_col = keep.tile([P, 4], BF16, name="b_col")

        b_rows = keep.tile([P, P], BF16, name="b_rows")
        nc.gpsimd.memset(b_rows[:], 0.0)
        nc.scalar.dma_start(out=b_rows[0:4, :], in_=bo.rearrange("(t c) -> t c", t=4))
        def load_a(i, pieces):
            rows = a_rows[512 * ORDER[i] : 512 * (ORDER[i] + 1), :].rearrange("(p s) k -> p s k", s=4)
            tiles = a_sb[i][:].rearrange("p (s k) -> p s k", s=4)
            for h in range(pieces):
                part = slice(4 // pieces * h, 4 // pieces * (h + 1))
                nc.sync.dma_start(out=tiles[:, part, :], in_=rows[:, part, :])

        def load_a_pair(i):
            g = ORDER[i]
            nc.sync.dma_start(
                out=a_pair[i][:],
                in_=a_rows[512 * g : 512 * (g + 2), :].rearrange("(p s) k -> p (s k)", s=8),
            )

        def load_x(i):
            if ORDER[i] == WRAP:
                nc.sync.dma_start(
                    out=x_sb[i][:].rearrange("q (r s) c -> q r (s c)", r=2),
                    in_=x_rows.rearrange("(r q s) c -> q r (s c)", r=16, s=2)[:, 0:16:15, :],
                )
            else:
                pix = 512 * ORDER[i] + 256
                nc.sync.dma_start(
                    out=x_sb[i][:], in_=x_rows[pix : pix + 512, :].rearrange("(q s) c -> q s c", s=4)
                )

        def load_x_pair(i):
            pix = 512 * ORDER[i] + 256
            nc.sync.dma_start(
                out=x_pair[i][:],
                in_=x_rows[pix : pix + 1024, :].rearrange("(q s) c -> q s c", s=8),
            )

        load_a(0, 2)
        nc.sync.dma_start(out=w_raw[:], in_=w_rows.rearrange("(p j) c -> p j c", j=4))
        load_a(1, 1)
        load_x(1)
        load_a_pair(2)
        load_x(0)
        load_x_pair(2)
        load_a_pair(4)
        load_x_pair(4)
        load_a_pair(6)
        load_x_pair(6)

        ident = keep.tile([P, P], F32, name="ident")
        make_identity(nc, ident[:])
        perm = keep.tile([P, P], F32, name="perm")
        src = ident[:].rearrange("p (a t h) -> p t a h", a=8, t=8, h=2)
        dst = perm[:].rearrange("p (t a h) -> p t a h", t=8, a=8, h=2)
        perm_wrap = keep.tile([P, P], F32, name="perm_wrap")
        src_w = ident[:].rearrange("p (a u t h) -> p u t a h", a=8, u=2, t=4, h=2)
        dst_w = perm_wrap[:].rearrange("p (v t a h) -> p v t a h", v=2, t=4, a=8, h=2)
        nc.vector.tensor_copy(out=dst[:, :, :, 1], in_=src[:, :, :, 0])
        nc.vector.tensor_copy(out=dst[:, :, 1:8, 0], in_=src[:, :, 0:7, 1])
        nc.vector.tensor_copy(out=dst[:, :, 0, 0], in_=src[:, :, 7, 1])
        for v in range(2):
            nc.vector.tensor_copy(out=dst_w[:, v, :, :, 1], in_=src_w[:, 1 - v, :, :, 0])
            nc.vector.tensor_copy(out=dst_w[:, v, :, 1:8, 0], in_=src_w[:, 1 - v, :, 0:7, 1])
            nc.vector.tensor_copy(out=dst_w[:, v, :, 0, 0], in_=src_w[:, 1 - v, :, 7, 1])
        perm_pair = []
        src_p = ident[:].rearrange("p (b a t) -> p b t a", b=2, a=8, t=8)
        for j in range(2):
            perm_j = keep.tile([P, P], F32, name="perm_pair%d" % j)
            perm_pair.append(perm_j)
            dst_p = perm_j[:].rearrange("p (b t a) -> p b t a", b=2, t=8, a=8)
            nc.vector.tensor_copy(out=dst_p[:, :, :, j:8], in_=src_p[:, :, :, 0 : 8 - j])
            if j == 1:
                nc.vector.tensor_copy(out=dst_p[:, :, :, 0], in_=src_p[:, :, :, 7])
        ident_bf = keep.tile([P, P], BF16, name="ident_bf")
        nc.vector.tensor_copy(out=ident_bf[:], in_=ident[:])

        warm_in = keep.tile([P, 1], F32, name="warm_in")
        warm_out = keep.tile([P, 1], F32, name="warm_out")
        nc.gpsimd.memset(warm_in[:], 0.0)
        nc.scalar.activation(out=warm_out[:], in_=warm_in[:], func=IDENTITY)

        w_grouped = keep.tile([P, 512, 4], BF16, name="w_grouped", align_bytes=64)
        w_codes = keep.tile([P, 512], U32, name="w_codes", align_bytes=64)
        w_scales = keep.tile([P, 512], U8, name="w_scales", align_bytes=64)
        b_bc = keep.tile([P, 512], F32, name="b_bc")

        def interleave_w(t, copy):
            cols = slice(P * t, P * (t + 1))
            copy(out=w_grouped[:, cols, :], in_=w_raw[:, :, cols].rearrange("p j c -> p c j"))

        def quantise_w(t):
            cols = slice(P * t, P * (t + 1))
            nc.vector.quantize_mx(
                out=w_codes[:, cols].bitcast(E4M3X4),
                scales=w_scales[:, cols],
                in_=w_grouped[:, cols, :].rearrange("p c j -> p (c j)"),
            )

        def bias_to_partitions():
            bt_ps = psum.tile([P, P], BF16, name="bank")
            nc.tensor.transpose(bt_ps[:], b_rows[:], ident_bf[:])
            nc.scalar.copy(out=b_col[:], in_=bt_ps[:, 0:4])

        def spread_bias():
            bb_ps = psum.tile([P, 512], BF16, name="bank")
            for t in range(4):
                nc.tensor.transpose(
                    bb_ps[:, P * t : P * (t + 1)], b_col[:, t : t + 1].to_broadcast([P, P]), ident_bf[:]
                )
            nc.vector.tensor_copy(out=b_bc[:], in_=bb_ps[:])

        def add_bias_to_x(i, half):
            tiles = slice(2 * half, 2 * half + 2)
            nc.vector.tensor_tensor(
                out=xb_sb[i][:, tiles, :],
                in0=x_sb[i][:, tiles, :],
                in1=b_bc[:].unsqueeze(1).to_broadcast([P, 2, 512]),
                op=ADD,
            )

        grouped = {}
        codes = {}
        scales = {}
        y_sb = {}

        def first_transposes(bank):
            i, h = divmod(bank, 2)
            words = a_sb[i][:].bitcast(F32)
            if h == 0:
                grouped[i] = work.tile([P, 2048], BF16, name="grouped", align_bytes=64)
            xt = psum.tile([P, 2, 2, P], F32, name="bank")
            wrap = ORDER[i] == WRAP
            order = perm if i == 0 else perm_wrap if i == 1 else perm_pair[i % 2]
            for a in range(2):
                s = h + 2 * a if wrap else 2 * h + a
                for u in range(2):
                    nc.tensor.transpose(
                        xt[:, a, u, :],
                        words[:, 256 * s + u : 256 * (s + 1) : 2],
                        order[:],
                    )
            if wrap:
                for v in range(2):
                    first = 512 * (2 * v + h)
                    nc.scalar.copy(
                        out=grouped[i][:, first : first + 512].bitcast(F32).rearrange("p (m a u) -> p m a u", a=2, u=2),
                        in_=xt[:, :, :, 64 * v : 64 * (v + 1)].rearrange("p a u m -> p m a u"),
                    )
            else:
                nc.scalar.copy(
                    out=grouped[i][:, 1024 * h : 1024 * (h + 1)]
                    .bitcast(F32)
                    .rearrange("p (a q u) -> p a q u", a=2, u=2),
                    in_=xt[:].rearrange("p a u q -> p a q u"),
                )

        def quantise(i):
            codes[i] = work.tile([P, 512], U32, name="codes", align_bytes=64)
            scales[i] = work.tile([P, 512], U8, name="scales", align_bytes=64)
            nc.vector.quantize_mx(out=codes[i][:].bitcast(E5M2X4), scales=scales[i][:], in_=grouped[i][:])

        def finished(i, s):
            if i == STRIPS - 1:
                pieces = 4
            elif i == 1 or i >= STRIPS - 4:
                pieces = 2
            else:
                pieces = 1
            tiles = 4 // pieces
            if (s + 1) % tiles != 0:
                return
            first = s + 1 - tiles
            if ORDER[i] == WRAP:
                pix = 0 if first == 0 else 3840
                rows = o_rows[pix : pix + 256, :].rearrange("(q s) c -> q s c", s=2)
            else:
                pix = 512 * ORDER[i] + 256
                if i == 0:
                    rows = o_rows[pix : pix + 512, :].rearrange("(q s) c -> q s c", s=4)[:, first : s + 1, :]
                else:
                    pix = pix - 512 * (i % 2)
                    slot = first + 4 * (1 - i % 2)
                    rows = o_rows[pix : pix + 1024, :].rearrange("(q s) c -> q s c", s=8)
                    rows = rows[:, slot : slot + s + 1 - first, :]
            nc.sync.dma_start(out=rows, in_=o_sb[i][:, first : s + 1, :])

        def product(i, r):
            cols = slice(P * r, P * (r + 1))
            bank = psum.tile([P, 512], F32, name="bank")
            if tokens_stationary(i):
                nc.tensor.matmul_mx(
                    out=bank[:],
                    lhsT=codes[i][:, cols].bitcast(E5M2X4),
                    lhsT_scale=scales[i][:, cols],
                    rhs=w_codes[:].bitcast(E4M3X4),
                    rhs_scale=w_scales[:],
                    start=True,
                    stop=True,
                )
                nc.vector.tensor_tensor(out=o_sb[i][:, r, :], in0=bank[:], in1=xb_sb[i][:, r, :], op=ADD)
                finished(i, r)
            else:
                if r == 0:
                    y_sb[i] = ybuf.tile([P, 4, 512], F32, name="y_sb")
                nc.tensor.matmul_mx(
                    out=bank[:],
                    lhsT=w_codes[:, cols].bitcast(E4M3X4),
                    lhsT_scale=w_scales[:, cols],
                    rhs=codes[i][:].bitcast(E5M2X4),
                    rhs_scale=scales[i][:],
                    start=True,
                    stop=True,
                )
                nc.scalar.activation(
                    out=y_sb[i][:, r, :], in_=bank[:], func=IDENTITY, bias=b_col[:, r : r + 1], scale=1.0
                )

        def turn_back(turns):
            banks = []
            for i, s in turns:
                bank = psum.tile([P, 512], F32, name="bank")
                banks.append(bank)
                if s != 1:
                    nc.tensor.matmul(out=bank[:], lhsT=ident_bf[:], rhs=x_sb[i][:, s, :], start=True, stop=False)
            for (i, s), bank in zip(turns, banks):
                if s != 1:
                    for t in range(4):
                        nc.tensor.matmul(
                            out=bank[:, P * t : P * (t + 1)],
                            lhsT=y_sb[i][:, t, P * s : P * (s + 1)],
                            rhs=ident[:],
                            is_transpose=True,
                            start=False,
                            stop=(t == 3),
                        )
                    nc.scalar.copy(out=o_sb[i][:, s, :], in_=bank[:])
                else:
                    for t in range(4):
                        nc.tensor.transpose(bank[:, P * t : P * (t + 1)], y_sb[i][:, t, P * s : P * (s + 1)], ident[:])
                    nc.vector.tensor_tensor(out=o_sb[i][:, s, :], in0=bank[:], in1=x_sb[i][:, s, :], op=ADD)
                finished(i, s)

        interleave_w(0, nc.vector.tensor_copy)
        interleave_w(1, nc.vector.tensor_copy)
        quantise_w(0)
        quantise_w(1)
        first_transposes(0)
        first_transposes(1)
        bias_to_partitions()
        quantise(0)
        spread_bias()
        interleave_w(2, nc.scalar.copy)
        interleave_w(3, nc.scalar.copy)
        first_transposes(2)
        first_transposes(3)
        quantise_w(2)
        quantise_w(3)
        add_bias_to_x(1, 0)
        to_turn = []
        for i in range(STRIPS):
            if i == STRIPS - 2:
                turn_back(to_turn)
                to_turn = []
            for r in range(4):
                product(i, r)
                if r == 1 and i + 1 < STRIPS:
                    quantise(i + 1)
                    if not tokens_stationary(i) and i > 0:
                        add_bias_to_x(i + 1, 0)
            if not tokens_stationary(i):
                add_bias_to_x(i + 1, 1)
            count = 2 if i + 1 < STRIPS else len(to_turn)
            turn_back(to_turn[:count])
            to_turn = to_turn[count:]
            if not tokens_stationary(i):
                to_turn.extend([(i, s) for s in range(4)])
            for bank in range(2 * i + AHEAD, 2 * i + AHEAD + 2):
                if bank < 2 * STRIPS:
                    first_transposes(bank)
